import numpy as np
import ml_dtypes

BF16 = ml_dtypes.bfloat16


def bf(x):
    return np.asarray(x, np.float32).astype(BF16)


def f32(x):
    return np.asarray(x, np.float32)


def f64(x):
    return np.asarray(x).astype(np.float64)


def striped(idx):
    return np.tile(idx.reshape(-1, 16).T, (8, 1))


D, S, N, HID, WIN = 128, 1024, 2048, 2048, 256
EPS = 1e-5


def layer_norm(z, gain, shift):
    m = z.mean(axis=0, keepdims=True)
    v = np.square(z - m).mean(axis=0, keepdims=True)
    return (z - m) / np.sqrt(v + EPS) * gain + shift


def setup_inputs():
    rn = np.random.standard_normal
    return {
        "table": bf(4.0 * rn((D, S))),
        "pos": bf(2.0 * rn((D, N))),
        "wq": bf(2.0 * rn((D, D)) / np.sqrt(D)),
        "bq": f32(0.3 * rn((D, 1))),
        "wk": bf(2.0 * rn((D, D)) / np.sqrt(D)),
        "wv": bf(2.0 * rn((D, D)) / np.sqrt(D)),
        "bv": f32(0.1 * rn((D, 1))),
        "wo": bf(4.0 * rn((D, D)) / np.sqrt(D)),
        "bo": f32(0.1 * rn((D, 1))),
        "wbias": f32(0.5 * rn((N, N))),
        "ln_gain": f32(1.0 + 0.1 * rn((D, 1))),
        "ln_shift": f32(0.1 * rn((D, 1))),
        "w1": bf(rn((D, HID)) / np.sqrt(D)),
        "b1": f32(0.1 * rn((HID, 1))),
        "w2": bf(rn((HID, D)) * np.sqrt(2.0 / HID)),
        "b2": f32(0.1 * rn((D, 1))),
        "offs": striped(np.concatenate([np.random.permutation(S)[:S // 2] for _ in range(N // (S // 2))])),
    }


def reference(table, pos, wq, bq, wk, wv, bv, wo, bo, wbias, ln_gain, ln_shift, w1, b1, w2, b2, offs):
    idx = offs[:16].T.reshape(-1)
    sc = 1.0 / np.sqrt(D)
    emb = sc * (f64(table)[:, idx] + 2.0 * f64(pos))
    qry = f64(wq).T @ emb + f64(bq)
    key = f64(wk).T @ emb
    val = f64(wv).T @ emb + f64(bv)
    t = np.arange(N)
    keep = (t[None, :] >= t[:, None]) & (t[None, :] - t[:, None] < WIN)
    ew = np.where(keep, np.exp(f64(wbias)), 0.0)
    ek = np.exp(key)
    num = (ek * val) @ ew
    den = ek @ ew
    y = (1.0 / (1.0 + np.exp(-qry))) * (num / den)
    att = f64(wo).T @ y + f64(bo)
    n1 = layer_norm(att + emb, f64(ln_gain), f64(ln_shift))
    hid = np.maximum(f64(w1).T @ n1 + f64(b1), 0.0)
    ffn = f64(w2).T @ hid + f64(b2)
    return layer_norm(ffn + n1, f64(ln_gain), f64(ln_shift))

@@ -1,0 +1,294 @@
+import math
+from contextlib import ExitStack
+
+import concourse.mybir as mybir
+from concourse.masks import make_identity
+
+BF16, F32, U16 = mybir.dt.bfloat16, mybir.dt.float32, mybir.dt.uint16
+ALU = mybir.AluOpType
+ACT = mybir.ActivationFunctionType
+
+P = 128
+S = 1024
+N = 2048
+HID = 2048
+WIN = 256
+EPS = 1e-5
+SC = 1.0 / math.sqrt(P)
+
+PIECE = 512
+N_PIECES = N // PIECE
+OFFS_COLS = PIECE // 16
+BLOCKS = N // P
+BLOCKS_PER_PIECE = PIECE // P
+BAND = WIN + P
+HID_BLOCKS = HID // P
+KEY, VAL, QRY = 0, 1, 2
+
+FLOPS = 2 * P * P * N * 4 + 2 * 2 * P * WIN * N + 2 * 2 * P * HID * N
+BYTES = (
+    2 * (P * S + P * N + 4 * P * P + 2 * P * HID)
+    + 4 * (6 * P + HID)
+    + 4 * (N * WIN - WIN * (WIN - 1) // 2)
+    + 2 * P * (N // 16)
+    + 4 * P * N
+)
+
+
+def tile_decoderonlyaft_b_kernel(
+    tc, table, pos, wq, bq, wk, wv, bv, wo, bo, wbias, ln_gain, ln_shift, w1, b1, w2, b2, offs, out
+):
+    nc = tc.nc
+    with ExitStack() as ctx:
+        ctx.enter_context(nc.allow_non_contiguous_dma(reason="b1 is loaded one value to a partition"))
+        held = ctx.enter_context(tc.tile_pool(name="held", bufs=1))
+        work = ctx.enter_context(tc.tile_pool(name="work", bufs=2))
+        hidden = ctx.enter_context(tc.tile_pool(name="hidden", bufs=6))
+        psum = ctx.enter_context(tc.psum_pool(name="psum", bufs=8))
+
+        def new_bank(name):
+            return psum.tile([P, PIECE], F32, name=name, tag="bank")
+
+        def piece(r):
+            return slice(r * PIECE, (r + 1) * PIECE)
+
+        def block(b):
+            return slice(b * P, (b + 1) * P)
+
+        offsets = held.tile([P, N // 16], U16, name="offsets")
+        nc.sync.dma_start(offsets[:], offs)
+        table_sb = held.tile([P, S], BF16, name="table_sb")
+        nc.sync.dma_start(table_sb[:], table)
+        w_qkv = held.tile([P, 3 * P], BF16, name="w_qkv")
+        for which, w in ((KEY, wk), (VAL, wv), (QRY, wq)):
+            nc.scalar.dma_start(w_qkv[:, block(which)], w)
+        pos_sb = held.tile([P, N], BF16, name="pos_sb")
+        nc.gpsimd.dma_start(pos_sb[:, 0 : N // 2], pos[:, 0 : N // 2])
+        nc.sync.dma_start(pos_sb[:, N // 2 : N], pos[:, N // 2 : N])
+
+        def load_vector(vec, name):
+            t = held.tile([P, 1], F32, name=name)
+            nc.scalar.dma_start(t[:], vec)
+            return t
+
+        bq_sb = load_vector(bq, "bq_sb")
+        bv_sb = load_vector(bv, "bv_sb")
+        bo_sb = load_vector(bo, "bo_sb")
+        b2_sb = load_vector(b2, "b2_sb")
+        gain = load_vector(ln_gain, "gain")
+        shift = load_vector(ln_shift, "shift")
+
+        band_cols = [min(BAND, N - P * u) for u in range(BLOCKS)]
+        wb = [held.tile([P, band_cols[u]], F32, name="wb%d" % u) for u in range(BLOCKS)]
+        for u in range(BLOCKS):
+            queue = nc.sync if u % 2 == 0 else nc.gpsimd
+            queue.dma_start(wb[u][:], wbias[block(u), u * P : u * P + band_cols[u]])
+
+        wo_sb = held.tile([P, P], BF16, name="wo_sb")
+        nc.sync.dma_start(wo_sb[:], wo)
+        w1_sb = held.tile([P, HID], BF16, name="w1_sb")
+        nc.sync.dma_start(w1_sb[:], w1)
+        w2_sb = held.tile([P, HID_BLOCKS, P], BF16, name="w2_sb")
+        nc.gpsimd.dma_start(w2_sb[:], w2.rearrange("(a p) c -> p a c", p=P))
+        b1_sb = held.tile([P, HID_BLOCKS], F32, name="b1_sb")
+        nc.scalar.dma_start(b1_sb[:], b1.rearrange("(a p) o -> p (a o)", p=P))
+
+        ident = held.tile([P, P], BF16, name="ident")
+        make_identity(nc, ident[:])
+        ident_f = held.tile([P, P], F32, name="ident_f")
+        make_identity(nc, ident_f[:])
+        center_f = held.tile([P, P], F32, name="center_f")
+        nc.vector.tensor_scalar(out=center_f[:], in0=ident_f[:], scalar1=-1.0 / P, scalar2=None, op0=ALU.add)
+        center = held.tile([P, P], BF16, name="center")
+        nc.vector.tensor_copy(center[:], center_f[:])
+        center2 = held.tile([P, P], BF16, name="center2")
+        nc.vector.tensor_scalar(out=center2[:], in0=center_f[:], scalar1=2.0, scalar2=None, op0=ALU.mult)
+        mean_w = held.tile([P, P], BF16, name="mean_w")
+        nc.vector.memset(mean_w[:], 1.0 / P)
+        eps1 = held.tile([P, 1], F32, name="eps1")
+        nc.vector.memset(eps1[:], EPS / (SC * SC))
+        eps2 = held.tile([P, 1], F32, name="eps2")
+        nc.vector.memset(eps2[:], EPS)
+
+        band_mask = held.tile([P, BAND], BF16, name="band_mask")
+        nc.gpsimd.memset(band_mask[:], 1.0)
+        nc.gpsimd.affine_select(
+            out=band_mask[:], in_=band_mask[:], compare_op=ALU.is_ge, fill=0.0,
+            base=0, pattern=[[1, BAND]], channel_multiplier=-1,
+        )
+        nc.gpsimd.affine_select(
+            out=band_mask[:], in_=band_mask[:], compare_op=ALU.is_ge, fill=0.0,
+            base=WIN - 1, pattern=[[-1, BAND]], channel_multiplier=1,
+        )
+
+        w_qkv2 = held.tile([P, 3 * P], BF16, name="w_qkv2")
+        nc.vector.tensor_scalar(out=w_qkv2[:], in0=w_qkv[:], scalar1=2.0, scalar2=None, op0=ALU.mult)
+        neg_bq = held.tile([P, 1], F32, name="neg_bq")
+        nc.vector.tensor_scalar(out=neg_bq[:], in0=bq_sb[:], scalar1=-1.0, scalar2=None, op0=ALU.mult)
+        bv_over_sc = held.tile([P, 1], F32, name="bv_over_sc")
+        nc.vector.tensor_scalar(out=bv_over_sc[:], in0=bv_sb[:], scalar1=1.0 / SC, scalar2=None, op0=ALU.mult)
+
+        wo_sum = held.tile([P, 1], F32, name="wo_sum")
+        nc.vector.tensor_reduce(out=wo_sum[:], in_=wo_sb[:], axis=mybir.AxisListType.X, op=ALU.add)
+        wo_mean = held.tile([P, 1], F32, name="wo_mean")
+        nc.vector.tensor_scalar(out=wo_mean[:], in0=wo_sum[:], scalar1=1.0 / P, scalar2=None, op0=ALU.mult)
+        wo_c = held.tile([P, P], BF16, name="wo_c")
+        nc.vector.tensor_scalar(out=wo_c[:], in0=wo_sb[:], scalar1=wo_mean[:, 0:1], scalar2=None, op0=ALU.subtract)
+        w2_sum = held.tile([P, HID_BLOCKS], F32, name="w2_sum")
+        nc.vector.tensor_reduce(out=w2_sum[:], in_=w2_sb[:], axis=mybir.AxisListType.X, op=ALU.add)
+        w2_negmean = held.tile([P, HID_BLOCKS], F32, name="w2_negmean")
+        nc.vector.tensor_scalar(out=w2_negmean[:], in0=w2_sum[:], scalar1=-1.0 / P, scalar2=None, op0=ALU.mult)
+        w2_c = held.tile([P, HID_BLOCKS, P], BF16, name="w2_c")
+        nc.gpsimd.tensor_tensor(
+            out=w2_c[:], in0=w2_sb[:], in1=w2_negmean[:].unsqueeze(2).to_broadcast([P, HID_BLOCKS, P]), op=ALU.add
+        )
+
+        z_bias_in = held.tile([P, 2], F32, name="z_bias_in")
+        nc.vector.tensor_scalar(out=z_bias_in[:, 0:1], in0=bo_sb[:], scalar1=1.0 / SC, scalar2=None, op0=ALU.mult)
+        nc.vector.tensor_copy(z_bias_in[:, 1:2], b2_sb[:])
+        z_bias_ps = new_bank("z_bias_ps")
+        nc.tensor.matmul(z_bias_ps[:, 0:2], center_f[:], z_bias_in[:], start=True, stop=True)
+        z_bias = held.tile([P, 2], F32, name="z_bias")
+        nc.vector.tensor_copy(z_bias[:], z_bias_ps[:, 0:2])
+
+        def project_pos(bank, which, r, start, stop):
+            nc.tensor.matmul(bank[:], w_qkv2[:, block(which)], pos_sb[:, piece(r)], start=start, stop=stop)
+
+        def project_table(bank, weights, r, start, stop):
+            looked_up = table_sb[:].indirect(offsets[:, r * OFFS_COLS : (r + 1) * OFFS_COLS])
+            nc.tensor.matmul(bank[:], weights, looked_up, start=start, stop=stop)
+
+        ek, ekv, eq, words = {}, {}, {}, {}
+
+        def finish(bank, which, r):
+            if which == KEY:
+                ek[r] = work.tile([P, PIECE], BF16, name="ek")
+                nc.scalar.activation(out=ek[r][:], in_=bank[:], func=ACT.Exp, scale=SC)
+            elif which == VAL:
+                ekv[r] = work.tile([P, PIECE], BF16, name="ekv")
+                nc.vector.scalar_tensor_tensor(
+                    out=ekv[r][:], in0=bank[:], scalar=bv_over_sc[:, 0:1], in1=ek[r][:], op0=ALU.add, op1=ALU.mult
+                )
+            else:
+                eq[r] = held.tile([P, PIECE], F32, name="eq%d" % r)
+                nc.scalar.activation(out=eq[r][:], in_=bank[:], func=ACT.Exp, scale=-SC, bias=neg_bq[:, 0:1])
+
+        kT = {}
+
+        def flip(r):
+            flipped = psum.tile([P, 2 * PIECE], BF16, name="flipped", tag="bank")
+            for b in range(BLOCKS_PER_PIECE):
+                nc.tensor.transpose(flipped[:, block(2 * b)], ekv[r][:, block(b)], ident[:])
+                nc.tensor.transpose(flipped[:, block(2 * b + 1)], ek[r][:, block(b)], ident[:])
+            kT[r] = held.tile([P, 2 * PIECE], BF16, name="kT%d" % r)
+            nc.vector.tensor_copy(kT[r][:], flipped[:])
+
+        order = ((KEY, VAL), (QRY,))
+        banks = {}
+        for r in (0, 1):
+            for which in (KEY, VAL, QRY):
+                banks[r, which] = new_bank("proj")
+                project_pos(banks[r, which], which, r, start=True, stop=False)
+        for group in order:
+            for r in (0, 1):
+                for which in group:
+                    project_table(banks[r, which], w_qkv[:, block(which)], r, start=False, stop=True)
+                    finish(banks[r, which], which, r)
+        for r in range(N_PIECES):
+            words_ps = new_bank("words_ps")
+            project_table(words_ps, ident[:], r, start=True, stop=True)
+            words[r] = held.tile([P, PIECE], BF16, name="words%d" % r)
+            nc.vector.tensor_copy(words[r][:], words_ps[:])
+        flip(0)
+        flip(1)
+        for group in order:
+            for r in (2, 3):
+                for which in group:
+                    banks[r, which] = new_bank("proj")
+                    project_table(banks[r, which], w_qkv[:, block(which)], r, start=True, stop=False)
+        for group in order:
+            for r in (2, 3):
+                for which in group:
+                    project_pos(banks[r, which], which, r, start=False, stop=True)
+                    finish(banks[r, which], which, r)
+        flip(2)
+        flip(3)
+
+        ew = []
+        for u in range(BLOCKS):
+            ew_raw = work.tile([P, BAND], BF16, name="ew_raw")
+            nc.scalar.activation(out=ew_raw[:, 0 : band_cols[u]], in_=wb[u][:], func=ACT.Exp)
+            ew.append(held.tile([P, band_cols[u]], BF16, name="ew%d" % u))
+            nc.gpsimd.tensor_tensor(
+                out=ew[u][:], in0=ew_raw[:, 0 : band_cols[u]], in1=band_mask[:, 0 : band_cols[u]], op=ALU.mult
+            )
+
+        y = {}
+        for r in range(N_PIECES):
+            num = new_bank("num")
+            den = new_bank("den")
+            for b in range(BLOCKS_PER_PIECE):
+                j = r * BLOCKS_PER_PIECE + b
+                attended = [u for u in (j - 2, j - 1, j) if u >= 0]
+                for u in attended:
+                    ur, ub = divmod(u, BLOCKS_PER_PIECE)
+                    seen = ew[u][:, block(j - u)]
+                    first, last = u == attended[0], u == attended[-1]
+                    nc.tensor.matmul(num[:, block(b)], kT[ur][:, block(2 * ub)], seen, start=first, stop=last)
+                    nc.tensor.matmul(den[:, block(b)], kT[ur][:, block(2 * ub + 1)], seen, start=first, stop=last)
+            divisor = work.tile([P, PIECE], F32, name="divisor")
+            nc.vector.scalar_tensor_tensor(
+                out=divisor[:], in0=eq[r][:], scalar=1.0, in1=den[:], op0=ALU.add, op1=ALU.mult
+            )
+            ln_divisor = work.tile([P, PIECE], F32, name="ln_divisor")
+            nc.scalar.activation(out=ln_divisor[:], in_=divisor[:], func=ACT.Ln)
+            inverse = work.tile([P, PIECE], F32, name="inverse")
+            nc.scalar.activation(out=inverse[:], in_=ln_divisor[:], func=ACT.Exp, scale=-1.0)
+            y[r] = held.tile([P, PIECE], BF16, name="y%d" % r)
+            nc.vector.tensor_tensor(out=y[r][:], in0=num[:], in1=inverse[:], op=ALU.mult)
+
+        def normalise(z, bias, eps):
+            squares = work.tile([P, PIECE], BF16, name="squares")
+            nc.scalar.activation(out=squares[:], in_=z[:], func=ACT.Square, bias=bias)
+            var = new_bank("var")
+            nc.tensor.matmul(var[:], mean_w[:], squares[:], start=True, stop=True)
+            ln_var = work.tile([P, PIECE], F32, name="ln_var")
+            nc.scalar.activation(out=ln_var[:], in_=var[:], func=ACT.Ln, bias=eps[:, 0:1])
+            rstd = work.tile([P, PIECE], F32, name="rstd")
+            nc.scalar.activation(out=rstd[:], in_=ln_var[:], func=ACT.Exp, scale=-0.5)
+            normed = work.tile([P, PIECE], F32, name="normed")
+            nc.vector.scalar_tensor_tensor(
+                out=normed[:], in0=z[:], scalar=bias, in1=rstd[:], op0=ALU.add, op1=ALU.mult
+            )
+            return normed
+
+        for r in range(N_PIECES):
+            z1 = new_bank("z1")
+            nc.tensor.matmul(z1[:], center[:], words[r][:], start=True, stop=False)
+            nc.tensor.matmul(z1[:], center2[:], pos_sb[:, piece(r)], start=False, stop=False)
+            nc.tensor.matmul(z1[:], wo_c[:], y[r][:], start=False, stop=True)
+            normed1 = normalise(z1, z_bias[:, 0:1], eps1)
+            n1 = work.tile([P, PIECE], BF16, name="n1")
+            nc.vector.tensor_scalar(
+                out=n1[:], in0=normed1[:], scalar1=gain[:, 0:1], scalar2=shift[:, 0:1], op0=ALU.mult, op1=ALU.add
+            )
+
+            z2 = new_bank("z2")
+            nc.tensor.matmul(z2[:], center[:], n1[:], start=True, stop=False)
+            for a in range(HID_BLOCKS):
+                hid_ps = new_bank("hid_ps")
+                nc.tensor.matmul(hid_ps[:], w1_sb[:, block(a)], n1[:], start=True, stop=True)
+                hid = hidden.tile([P, PIECE], BF16, name="hid")
+                if a % 2 == 0:
+                    nc.scalar.activation(out=hid[:], in_=hid_ps[:], func=ACT.Relu, bias=b1_sb[:, a : a + 1])
+                else:
+                    nc.vector.tensor_scalar(
+                        out=hid[:], in0=hid_ps[:], scalar1=b1_sb[:, a : a + 1], scalar2=0.0, op0=ALU.add, op1=ALU.max
+                    )
+                nc.tensor.matmul(z2[:], w2_c[:, a, :], hid[:], start=False, stop=(a == HID_BLOCKS - 1))
+            normed2 = normalise(z2, z_bias[:, 1:2], eps2)
+            result = work.tile([P, PIECE], F32, name="result")
+            nc.gpsimd.tensor_scalar(
+                out=result[:], in0=normed2[:], scalar1=gain[:, 0:1], scalar2=shift[:, 0:1], op0=ALU.mult, op1=ALU.add
+            )
+            nc.sync.dma_start(out[:, piece(r)], result[:])

@@ -24,6 +24,7 @@ BLOCKS_PER_PIECE = PIECE // P
 BAND = WIN + P
 HID_BLOCKS = HID // P
 KEY, VAL, QRY = 0, 1, 2
+AHEAD = 3
 
 FLOPS = 2 * P * P * N * 4 + 2 * 2 * P * WIN * N + 2 * 2 * P * HID * N
 BYTES = (
@@ -42,7 +43,7 @@ def tile_decoderonlyaft_b_kernel(
     with ExitStack() as ctx:
         ctx.enter_context(nc.allow_non_contiguous_dma(reason="b1 is loaded one value to a partition"))
         held = ctx.enter_context(tc.tile_pool(name="held", bufs=1))
-        work = ctx.enter_context(tc.tile_pool(name="work", bufs=2))
+        work = ctx.enter_context(tc.tile_pool(name="work", bufs=4))
         hidden = ctx.enter_context(tc.tile_pool(name="hidden", bufs=6))
         psum = ctx.enter_context(tc.psum_pool(name="psum", bufs=8))
 
@@ -55,24 +56,24 @@ def tile_decoderonlyaft_b_kernel(
         def block(b):
             return slice(b * P, (b + 1) * P)
 
+        pos_sb = held.tile([P, N], BF16, name="pos_sb")
+        nc.sync.dma_start(pos_sb[:, 0 : N // 2], pos[:, 0 : N // 2])
+        w_qkv = held.tile([P, 3 * P], BF16, name="w_qkv")
+        for which, w in ((KEY, wk), (VAL, wv), (QRY, wq)):
+            nc.scalar.dma_start(w_qkv[:, block(which)], w)
         offsets = held.tile([P, N // 16], U16, name="offsets")
         nc.sync.dma_start(offsets[:], offs)
         table_sb = held.tile([P, S], BF16, name="table_sb")
         nc.sync.dma_start(table_sb[:], table)
-        w_qkv = held.tile([P, 3 * P], BF16, name="w_qkv")
-        for which, w in ((KEY, wk), (VAL, wv), (QRY, wq)):
-            nc.scalar.dma_start(w_qkv[:, block(which)], w)
-        pos_sb = held.tile([P, N], BF16, name="pos_sb")
-        nc.gpsimd.dma_start(pos_sb[:, 0 : N // 2], pos[:, 0 : N // 2])
         nc.sync.dma_start(pos_sb[:, N // 2 : N], pos[:, N // 2 : N])
 
         def load_vector(vec, name):
             t = held.tile([P, 1], F32, name=name)
-            nc.scalar.dma_start(t[:], vec)
+            nc.gpsimd.dma_start(t[:], vec)
             return t
 
-        bq_sb = load_vector(bq, "bq_sb")
         bv_sb = load_vector(bv, "bv_sb")
+        bq_sb = load_vector(bq, "bq_sb")
         bo_sb = load_vector(bo, "bo_sb")
         b2_sb = load_vector(b2, "b2_sb")
         gain = load_vector(ln_gain, "gain")
@@ -81,17 +82,17 @@ def tile_decoderonlyaft_b_kernel(
         band_cols = [min(BAND, N - P * u) for u in range(BLOCKS)]
         wb = [held.tile([P, band_cols[u]], F32, name="wb%d" % u) for u in range(BLOCKS)]
         for u in range(BLOCKS):
-            queue = nc.sync if u % 2 == 0 else nc.gpsimd
+            queue = nc.sync if u % 2 == 0 else nc.scalar
             queue.dma_start(wb[u][:], wbias[block(u), u * P : u * P + band_cols[u]])
 
         wo_sb = held.tile([P, P], BF16, name="wo_sb")
-        nc.sync.dma_start(wo_sb[:], wo)
+        nc.gpsimd.dma_start(wo_sb[:], wo)
         w1_sb = held.tile([P, HID], BF16, name="w1_sb")
-        nc.sync.dma_start(w1_sb[:], w1)
+        nc.gpsimd.dma_start(w1_sb[:], w1)
         w2_sb = held.tile([P, HID_BLOCKS, P], BF16, name="w2_sb")
         nc.gpsimd.dma_start(w2_sb[:], w2.rearrange("(a p) c -> p a c", p=P))
         b1_sb = held.tile([P, HID_BLOCKS], F32, name="b1_sb")
-        nc.scalar.dma_start(b1_sb[:], b1.rearrange("(a p) o -> p (a o)", p=P))
+        nc.gpsimd.dma_start(b1_sb[:], b1.rearrange("(a p) o -> p (a o)", p=P))
 
         ident = held.tile([P, P], BF16, name="ident")
         make_identity(nc, ident[:])
@@ -110,15 +111,15 @@ def tile_decoderonlyaft_b_kernel(
         eps2 = held.tile([P, 1], F32, name="eps2")
         nc.vector.memset(eps2[:], EPS)
 
-        band_mask = held.tile([P, BAND], BF16, name="band_mask")
-        nc.gpsimd.memset(band_mask[:], 1.0)
+        edge_mask = held.tile([P, 2, P], BF16, name="edge_mask")
+        nc.gpsimd.memset(edge_mask[:], 1.0)
         nc.gpsimd.affine_select(
-            out=band_mask[:], in_=band_mask[:], compare_op=ALU.is_ge, fill=0.0,
-            base=0, pattern=[[1, BAND]], channel_multiplier=-1,
+            out=edge_mask[:, 0, :], in_=edge_mask[:, 0, :], compare_op=ALU.is_ge, fill=0.0,
+            base=0, pattern=[[1, P]], channel_multiplier=-1,
         )
         nc.gpsimd.affine_select(
-            out=band_mask[:], in_=band_mask[:], compare_op=ALU.is_ge, fill=0.0,
-            base=WIN - 1, pattern=[[-1, BAND]], channel_multiplier=1,
+            out=edge_mask[:, 1, :], in_=edge_mask[:, 1, :], compare_op=ALU.is_gt, fill=0.0,
+            base=0, pattern=[[-1, P]], channel_multiplier=1,
         )
 
         w_qkv2 = held.tile([P, 3 * P], BF16, name="w_qkv2")
@@ -142,14 +143,6 @@ def tile_decoderonlyaft_b_kernel(
         nc.gpsimd.tensor_tensor(
             out=w2_c[:], in0=w2_sb[:], in1=w2_negmean[:].unsqueeze(2).to_broadcast([P, HID_BLOCKS, P]), op=ALU.add
         )
-
-        z_bias_in = held.tile([P, 2], F32, name="z_bias_in")
-        nc.vector.tensor_scalar(out=z_bias_in[:, 0:1], in0=bo_sb[:], scalar1=1.0 / SC, scalar2=None, op0=ALU.mult)
-        nc.vector.tensor_copy(z_bias_in[:, 1:2], b2_sb[:])
-        z_bias_ps = new_bank("z_bias_ps")
-        nc.tensor.matmul(z_bias_ps[:, 0:2], center_f[:], z_bias_in[:], start=True, stop=True)
-        z_bias = held.tile([P, 2], F32, name="z_bias")
-        nc.vector.tensor_copy(z_bias[:], z_bias_ps[:, 0:2])
 
         def project_pos(bank, which, r, start, stop):
             nc.tensor.matmul(bank[:], w_qkv2[:, block(which)], pos_sb[:, piece(r)], start=start, stop=stop)
@@ -216,15 +209,25 @@ def tile_decoderonlyaft_b_kernel(
 
         ew = []
         for u in range(BLOCKS):
-            ew_raw = work.tile([P, BAND], BF16, name="ew_raw")
-            nc.scalar.activation(out=ew_raw[:, 0 : band_cols[u]], in_=wb[u][:], func=ACT.Exp)
             ew.append(held.tile([P, band_cols[u]], BF16, name="ew%d" % u))
-            nc.gpsimd.tensor_tensor(
-                out=ew[u][:], in0=ew_raw[:, 0 : band_cols[u]], in1=band_mask[:, 0 : band_cols[u]], op=ALU.mult
-            )
+            nc.scalar.activation(out=ew[u][:], in_=wb[u][:], func=ACT.Exp)
+            nc.vector.tensor_tensor(out=ew[u][:, block(0)], in0=ew[u][:, block(0)], in1=edge_mask[:, 0, :], op=ALU.mult)
+            if band_cols[u] == BAND:
+                nc.vector.tensor_tensor(
+                    out=ew[u][:, block(2)], in0=ew[u][:, block(2)], in1=edge_mask[:, 1, :], op=ALU.mult
+                )
+
+        z_bias_in = held.tile([P, 2], F32, name="z_bias_in")
+        nc.vector.tensor_scalar(out=z_bias_in[:, 0:1], in0=bo_sb[:], scalar1=1.0 / SC, scalar2=None, op0=ALU.mult)
+        nc.vector.tensor_copy(z_bias_in[:, 1:2], b2_sb[:])
+        z_bias_ps = new_bank("z_bias_ps")
+        nc.tensor.matmul(z_bias_ps[:, 0:2], center_f[:], z_bias_in[:], start=True, stop=True)
+        z_bias = held.tile([P, 2], F32, name="z_bias")
+        nc.vector.tensor_copy(z_bias[:], z_bias_ps[:, 0:2])
 
         y = {}
-        for r in range(N_PIECES):
+
+        def mix(r):
             num = new_bank("num")
             den = new_bank("den")
             for b in range(BLOCKS_PER_PIECE):
@@ -240,10 +243,10 @@ def tile_decoderonlyaft_b_kernel(
             nc.vector.scalar_tensor_tensor(
                 out=divisor[:], in0=eq[r][:], scalar=1.0, in1=den[:], op0=ALU.add, op1=ALU.mult
             )
-            ln_divisor = work.tile([P, PIECE], F32, name="ln_divisor")
-            nc.scalar.activation(out=ln_divisor[:], in_=divisor[:], func=ACT.Ln)
+            inverse_root = work.tile([P, PIECE], F32, name="inverse_root")
+            nc.scalar.activation(out=inverse_root[:], in_=divisor[:], func=ACT.Abs_reciprocal_sqrt)
             inverse = work.tile([P, PIECE], F32, name="inverse")
-            nc.scalar.activation(out=inverse[:], in_=ln_divisor[:], func=ACT.Exp, scale=-1.0)
+            nc.scalar.activation(out=inverse[:], in_=inverse_root[:], func=ACT.Square)
             y[r] = held.tile([P, PIECE], BF16, name="y%d" % r)
             nc.vector.tensor_tensor(out=y[r][:], in0=num[:], in1=inverse[:], op=ALU.mult)
 
@@ -252,43 +255,56 @@ def tile_decoderonlyaft_b_kernel(
             nc.scalar.activation(out=squares[:], in_=z[:], func=ACT.Square, bias=bias)
             var = new_bank("var")
             nc.tensor.matmul(var[:], mean_w[:], squares[:], start=True, stop=True)
-            ln_var = work.tile([P, PIECE], F32, name="ln_var")
-            nc.scalar.activation(out=ln_var[:], in_=var[:], func=ACT.Ln, bias=eps[:, 0:1])
             rstd = work.tile([P, PIECE], F32, name="rstd")
-            nc.scalar.activation(out=rstd[:], in_=ln_var[:], func=ACT.Exp, scale=-0.5)
+            nc.scalar.activation(out=rstd[:], in_=var[:], func=ACT.Abs_reciprocal_sqrt, bias=eps[:, 0:1])
             normed = work.tile([P, PIECE], F32, name="normed")
             nc.vector.scalar_tensor_tensor(
                 out=normed[:], in0=z[:], scalar=bias, in1=rstd[:], op0=ALU.add, op1=ALU.mult
             )
             return normed
 
-        for r in range(N_PIECES):
+        n1 = {}
+
+        def first_norm(r):
             z1 = new_bank("z1")
             nc.tensor.matmul(z1[:], center[:], words[r][:], start=True, stop=False)
             nc.tensor.matmul(z1[:], center2[:], pos_sb[:, piece(r)], start=False, stop=False)
             nc.tensor.matmul(z1[:], wo_c[:], y[r][:], start=False, stop=True)
             normed1 = normalise(z1, z_bias[:, 0:1], eps1)
-            n1 = work.tile([P, PIECE], BF16, name="n1")
+            n1[r] = held.tile([P, PIECE], BF16, name="n1_%d" % r)
             nc.vector.tensor_scalar(
-                out=n1[:], in0=normed1[:], scalar1=gain[:, 0:1], scalar2=shift[:, 0:1], op0=ALU.mult, op1=ALU.add
+                out=n1[r][:], in0=normed1[:], scalar1=gain[:, 0:1], scalar2=shift[:, 0:1], op0=ALU.mult, op1=ALU.add
             )
 
+        def feed_forward(r):
             z2 = new_bank("z2")
-            nc.tensor.matmul(z2[:], center[:], n1[:], start=True, stop=False)
-            for a in range(HID_BLOCKS):
-                hid_ps = new_bank("hid_ps")
-                nc.tensor.matmul(hid_ps[:], w1_sb[:, block(a)], n1[:], start=True, stop=True)
-                hid = hidden.tile([P, PIECE], BF16, name="hid")
-                if a % 2 == 0:
-                    nc.scalar.activation(out=hid[:], in_=hid_ps[:], func=ACT.Relu, bias=b1_sb[:, a : a + 1])
-                else:
-                    nc.vector.tensor_scalar(
-                        out=hid[:], in0=hid_ps[:], scalar1=b1_sb[:, a : a + 1], scalar2=0.0, op0=ALU.add, op1=ALU.max
-                    )
-                nc.tensor.matmul(z2[:], w2_c[:, a, :], hid[:], start=False, stop=(a == HID_BLOCKS - 1))
+            nc.tensor.matmul(z2[:], center[:], n1[r][:], start=True, stop=False)
+            hid = {}
+            for a in range(HID_BLOCKS + AHEAD):
+                if a < HID_BLOCKS:
+                    hid_ps = new_bank("hid_ps")
+                    nc.tensor.matmul(hid_ps[:], w1_sb[:, block(a)], n1[r][:], start=True, stop=True)
+                    hid[a] = hidden.tile([P, PIECE], BF16, name="hid")
+                    if a % 3 == 0:
+                        nc.scalar.activation(out=hid[a][:], in_=hid_ps[:], func=ACT.Relu, bias=b1_sb[:, a : a + 1])
+                    else:
+                        nc.vector.tensor_scalar(
+                            out=hid[a][:], in0=hid_ps[:], scalar1=b1_sb[:, a : a + 1], scalar2=0.0,
+                            op0=ALU.add, op1=ALU.max,
+                        )
+                if a >= AHEAD:
+                    done = a - AHEAD
+                    nc.tensor.matmul(z2[:], w2_c[:, done, :], hid[done][:], start=False, stop=(done == HID_BLOCKS - 1))
             normed2 = normalise(z2, z_bias[:, 1:2], eps2)
             result = work.tile([P, PIECE], F32, name="result")
-            nc.gpsimd.tensor_scalar(
+            nc.vector.tensor_scalar(
                 out=result[:], in0=normed2[:], scalar1=gain[:, 0:1], scalar2=shift[:, 0:1], op0=ALU.mult, op1=ALU.add
             )
             nc.sync.dma_start(out[:, piece(r)], result[:])
+
+        for r in range(N_PIECES + 2):
+            if r < N_PIECES:
+                mix(r)
+                first_norm(r)
+            if r >= 2:
+                feed_forward(r - 2)

@@ -24,7 +24,8 @@ BLOCKS_PER_PIECE = PIECE // P
 BAND = WIN + P
 HID_BLOCKS = HID // P
 KEY, VAL, QRY = 0, 1, 2
-AHEAD = 3
+AHEAD = 4
+EARLY_BAND_BLOCKS = 12
 
 FLOPS = 2 * P * P * N * 4 + 2 * 2 * P * WIN * N + 2 * 2 * P * HID * N
 BYTES = (
@@ -56,60 +57,47 @@ def tile_decoderonlyaft_b_kernel(
         def block(b):
             return slice(b * P, (b + 1) * P)
 
-        pos_sb = held.tile([P, N], BF16, name="pos_sb")
-        nc.sync.dma_start(pos_sb[:, 0 : N // 2], pos[:, 0 : N // 2])
-        w_qkv = held.tile([P, 3 * P], BF16, name="w_qkv")
-        for which, w in ((KEY, wk), (VAL, wv), (QRY, wq)):
-            nc.scalar.dma_start(w_qkv[:, block(which)], w)
-        offsets = held.tile([P, N // 16], U16, name="offsets")
-        nc.sync.dma_start(offsets[:], offs)
-        table_sb = held.tile([P, S], BF16, name="table_sb")
-        nc.sync.dma_start(table_sb[:], table)
-        nc.sync.dma_start(pos_sb[:, N // 2 : N], pos[:, N // 2 : N])
-
-        def load_vector(vec, name):
-            t = held.tile([P, 1], F32, name=name)
-            nc.gpsimd.dma_start(t[:], vec)
+        def load(queue, shape, dtype, name, source):
+            t = held.tile(shape, dtype, name=name)
+            queue.dma_start(t[:], source)
             return t
 
-        bv_sb = load_vector(bv, "bv_sb")
-        bq_sb = load_vector(bq, "bq_sb")
-        bo_sb = load_vector(bo, "bo_sb")
-        b2_sb = load_vector(b2, "b2_sb")
-        gain = load_vector(ln_gain, "gain")
-        shift = load_vector(ln_shift, "shift")
+        def load_band(queue, m):
+            first = 2 * P * m
+            cols = min(4 * P, N - first)
+            source = wbias[first : first + 2 * P, first : first + cols].rearrange("(a p) x -> p a x", p=P)
+            return load(queue, [P, 2, cols], F32, "wb%d" % m, source)
 
-        band_cols = [min(BAND, N - P * u) for u in range(BLOCKS)]
-        wb = [held.tile([P, band_cols[u]], F32, name="wb%d" % u) for u in range(BLOCKS)]
-        for u in range(BLOCKS):
-            queue = nc.sync if u % 2 == 0 else nc.scalar
-            queue.dma_start(wb[u][:], wbias[block(u), u * P : u * P + band_cols[u]])
-
-        wo_sb = held.tile([P, P], BF16, name="wo_sb")
-        nc.gpsimd.dma_start(wo_sb[:], wo)
-        w1_sb = held.tile([P, HID], BF16, name="w1_sb")
-        nc.gpsimd.dma_start(w1_sb[:], w1)
-        w2_sb = held.tile([P, HID_BLOCKS, P], BF16, name="w2_sb")
-        nc.gpsimd.dma_start(w2_sb[:], w2.rearrange("(a p) c -> p a c", p=P))
-        b1_sb = held.tile([P, HID_BLOCKS], F32, name="b1_sb")
-        nc.gpsimd.dma_start(b1_sb[:], b1.rearrange("(a p) o -> p (a o)", p=P))
-
+        w_sb = {}
+        pos_sb = load(nc.sync, [P, N], BF16, "pos_sb", pos)
+        w_sb[KEY] = load(nc.scalar, [P, P], BF16, "wk_sb", wk)
+        w_sb[VAL] = load(nc.gpsimd, [P, P], BF16, "wv_sb", wv)
+        offsets = held.tile([P, N // 16], U16, name="offsets")
+        nc.sync.dma_start(offsets[:], offs)
+        w_sb[QRY] = load(nc.scalar, [P, P], BF16, "wq_sb", wq)
+        table_sb = load(nc.gpsimd, [P, S], BF16, "table_sb", table)
         ident = held.tile([P, P], BF16, name="ident")
         make_identity(nc, ident[:])
-        ident_f = held.tile([P, P], F32, name="ident_f")
-        make_identity(nc, ident_f[:])
-        center_f = held.tile([P, P], F32, name="center_f")
-        nc.vector.tensor_scalar(out=center_f[:], in0=ident_f[:], scalar1=-1.0 / P, scalar2=None, op0=ALU.add)
-        center = held.tile([P, P], BF16, name="center")
-        nc.vector.tensor_copy(center[:], center_f[:])
-        center2 = held.tile([P, P], BF16, name="center2")
-        nc.vector.tensor_scalar(out=center2[:], in0=center_f[:], scalar1=2.0, scalar2=None, op0=ALU.mult)
-        mean_w = held.tile([P, P], BF16, name="mean_w")
-        nc.vector.memset(mean_w[:], 1.0 / P)
-        eps1 = held.tile([P, 1], F32, name="eps1")
-        nc.vector.memset(eps1[:], EPS / (SC * SC))
-        eps2 = held.tile([P, 1], F32, name="eps2")
-        nc.vector.memset(eps2[:], EPS)
+        bv_sb = load(nc.scalar, [P, 1], F32, "bv_sb", bv)
+        bq_sb = load(nc.gpsimd, [P, 1], F32, "bq_sb", bq)
+        wb = [load_band(nc.scalar if m % 2 == 0 else nc.sync, m) for m in range(BLOCKS // 2)]
+        w2_sb = load(nc.gpsimd, [P, HID_BLOCKS, P], BF16, "w2_sb", w2.rearrange("(a p) c -> p a c", p=P))
+        bo_sb = load(nc.gpsimd, [P, 1], F32, "bo_sb", bo)
+        wo_sb = load(nc.sync, [P, P], BF16, "wo_sb", wo)
+        gain = load(nc.scalar, [P, 1], F32, "gain", ln_gain)
+        b1_sb = load(nc.gpsimd, [P, HID_BLOCKS], F32, "b1_sb", b1.rearrange("(a p) o -> p (a o)", p=P))
+        w1_sb = load(nc.sync, [P, HID], BF16, "w1_sb", w1)
+        shift = load(nc.scalar, [P, 1], F32, "shift", ln_shift)
+        b2_sb = load(nc.gpsimd, [P, 1], F32, "b2_sb", b2)
+
+        w_twice = {}
+        for which in (KEY, VAL, QRY):
+            w_twice[which] = held.tile([P, P], BF16, name="w_twice%d" % which)
+            nc.vector.tensor_scalar(out=w_twice[which][:], in0=w_sb[which][:], scalar1=2.0, scalar2=None, op0=ALU.mult)
+        bv_over_sc = held.tile([P, 1], F32, name="bv_over_sc")
+        nc.vector.tensor_scalar(out=bv_over_sc[:], in0=bv_sb[:], scalar1=1.0 / SC, scalar2=None, op0=ALU.mult)
+        neg_bq = held.tile([P, 1], F32, name="neg_bq")
+        nc.vector.tensor_scalar(out=neg_bq[:], in0=bq_sb[:], scalar1=-1.0, scalar2=None, op0=ALU.mult)
 
         edge_mask = held.tile([P, 2, P], BF16, name="edge_mask")
         nc.gpsimd.memset(edge_mask[:], 1.0)
@@ -121,31 +109,11 @@ def tile_decoderonlyaft_b_kernel(
             out=edge_mask[:, 1, :], in_=edge_mask[:, 1, :], compare_op=ALU.is_gt, fill=0.0,
             base=0, pattern=[[-1, P]], channel_multiplier=1,
         )
-
-        w_qkv2 = held.tile([P, 3 * P], BF16, name="w_qkv2")
-        nc.vector.tensor_scalar(out=w_qkv2[:], in0=w_qkv[:], scalar1=2.0, scalar2=None, op0=ALU.mult)
-        neg_bq = held.tile([P, 1], F32, name="neg_bq")
-        nc.vector.tensor_scalar(out=neg_bq[:], in0=bq_sb[:], scalar1=-1.0, scalar2=None, op0=ALU.mult)
-        bv_over_sc = held.tile([P, 1], F32, name="bv_over_sc")
-        nc.vector.tensor_scalar(out=bv_over_sc[:], in0=bv_sb[:], scalar1=1.0 / SC, scalar2=None, op0=ALU.mult)
-
-        wo_sum = held.tile([P, 1], F32, name="wo_sum")
-        nc.vector.tensor_reduce(out=wo_sum[:], in_=wo_sb[:], axis=mybir.AxisListType.X, op=ALU.add)
-        wo_mean = held.tile([P, 1], F32, name="wo_mean")
-        nc.vector.tensor_scalar(out=wo_mean[:], in0=wo_sum[:], scalar1=1.0 / P, scalar2=None, op0=ALU.mult)
-        wo_c = held.tile([P, P], BF16, name="wo_c")
-        nc.vector.tensor_scalar(out=wo_c[:], in0=wo_sb[:], scalar1=wo_mean[:, 0:1], scalar2=None, op0=ALU.subtract)
-        w2_sum = held.tile([P, HID_BLOCKS], F32, name="w2_sum")
-        nc.vector.tensor_reduce(out=w2_sum[:], in_=w2_sb[:], axis=mybir.AxisListType.X, op=ALU.add)
-        w2_negmean = held.tile([P, HID_BLOCKS], F32, name="w2_negmean")
-        nc.vector.tensor_scalar(out=w2_negmean[:], in0=w2_sum[:], scalar1=-1.0 / P, scalar2=None, op0=ALU.mult)
-        w2_c = held.tile([P, HID_BLOCKS, P], BF16, name="w2_c")
-        nc.gpsimd.tensor_tensor(
-            out=w2_c[:], in0=w2_sb[:], in1=w2_negmean[:].unsqueeze(2).to_broadcast([P, HID_BLOCKS, P]), op=ALU.add
-        )
+        ident_f = held.tile([P, P], F32, name="ident_f")
+        make_identity(nc, ident_f[:])
 
         def project_pos(bank, which, r, start, stop):
-            nc.tensor.matmul(bank[:], w_qkv2[:, block(which)], pos_sb[:, piece(r)], start=start, stop=stop)
+            nc.tensor.matmul(bank[:], w_twice[which][:], pos_sb[:, piece(r)], start=start, stop=stop)
 
         def project_table(bank, weights, r, start, stop):
             looked_up = table_sb[:].indirect(offsets[:, r * OFFS_COLS : (r + 1) * OFFS_COLS])
@@ -176,16 +144,30 @@ def tile_decoderonlyaft_b_kernel(
             kT[r] = held.tile([P, 2 * PIECE], BF16, name="kT%d" % r)
             nc.vector.tensor_copy(kT[r][:], flipped[:])
 
+        band_cols = [min(BAND, N - P * u) for u in range(BLOCKS)]
+        ew = {}
+
+        def band_weights(u):
+            m, a = divmod(u, 2)
+            ew[u] = held.tile([P, band_cols[u]], BF16, name="ew%d" % u)
+            nc.scalar.activation(out=ew[u][:], in_=wb[m][:, a, a * P : a * P + band_cols[u]], func=ACT.Exp)
+            nc.vector.tensor_tensor(out=ew[u][:, block(0)], in0=ew[u][:, block(0)], in1=edge_mask[:, 0, :], op=ALU.mult)
+            if band_cols[u] == BAND:
+                nc.vector.tensor_tensor(
+                    out=ew[u][:, block(2)], in0=ew[u][:, block(2)], in1=edge_mask[:, 1, :], op=ALU.mult
+                )
+
         order = ((KEY, VAL), (QRY,))
         banks = {}
-        for r in (0, 1):
-            for which in (KEY, VAL, QRY):
-                banks[r, which] = new_bank("proj")
-                project_pos(banks[r, which], which, r, start=True, stop=False)
         for group in order:
             for r in (0, 1):
                 for which in group:
-                    project_table(banks[r, which], w_qkv[:, block(which)], r, start=False, stop=True)
+                    banks[r, which] = new_bank("proj")
+                    project_pos(banks[r, which], which, r, start=True, stop=False)
+        for group in order:
+            for r in (0, 1):
+                for which in group:
+                    project_table(banks[r, which], w_sb[which][:], r, start=False, stop=True)
                     finish(banks[r, which], which, r)
         for r in range(N_PIECES):
             words_ps = new_bank("words_ps")
@@ -198,37 +180,64 @@ def tile_decoderonlyaft_b_kernel(
             for r in (2, 3):
                 for which in group:
                     banks[r, which] = new_bank("proj")
-                    project_table(banks[r, which], w_qkv[:, block(which)], r, start=True, stop=False)
+                    project_table(banks[r, which], w_sb[which][:], r, start=True, stop=False)
+
+        for u in range(EARLY_BAND_BLOCKS):
+            band_weights(u)
+        center_f = held.tile([P, P], F32, name="center_f")
+        nc.vector.tensor_scalar(out=center_f[:], in0=ident_f[:], scalar1=-1.0 / P, scalar2=None, op0=ALU.add)
+        center = held.tile([P, P], BF16, name="center")
+        nc.vector.tensor_copy(center[:], center_f[:])
+        center2 = held.tile([P, P], BF16, name="center2")
+        nc.vector.tensor_scalar(out=center2[:], in0=center_f[:], scalar1=2.0, scalar2=None, op0=ALU.mult)
+        mean_w = held.tile([P, P], BF16, name="mean_w")
+        nc.vector.memset(mean_w[:], 1.0 / P)
+        eps1 = held.tile([P, 1], F32, name="eps1")
+        nc.vector.memset(eps1[:], EPS / (SC * SC))
+        eps2 = held.tile([P, 1], F32, name="eps2")
+        nc.vector.memset(eps2[:], EPS)
+        w2_sum = held.tile([P, HID_BLOCKS], F32, name="w2_sum")
+        nc.vector.tensor_reduce(out=w2_sum[:], in_=w2_sb[:], axis=mybir.AxisListType.X, op=ALU.add)
+        w2_negmean = held.tile([P, HID_BLOCKS], F32, name="w2_negmean")
+        nc.vector.tensor_scalar(out=w2_negmean[:], in0=w2_sum[:], scalar1=-1.0 / P, scalar2=None, op0=ALU.mult)
+        w2_c = held.tile([P, HID_BLOCKS, P], BF16, name="w2_c")
+        nc.gpsimd.tensor_tensor(
+            out=w2_c[:], in0=w2_sb[:], in1=w2_negmean[:].unsqueeze(2).to_broadcast([P, HID_BLOCKS, P]), op=ALU.add
+        )
+
         for group in order:
             for r in (2, 3):
                 for which in group:
                     project_pos(banks[r, which], which, r, start=False, stop=True)
                     finish(banks[r, which], which, r)
-        flip(2)
-        flip(3)
+        for u in range(EARLY_BAND_BLOCKS, BLOCKS):
+            band_weights(u)
 
-        ew = []
-        for u in range(BLOCKS):
-            ew.append(held.tile([P, band_cols[u]], BF16, name="ew%d" % u))
-            nc.scalar.activation(out=ew[u][:], in_=wb[u][:], func=ACT.Exp)
-            nc.vector.tensor_tensor(out=ew[u][:, block(0)], in0=ew[u][:, block(0)], in1=edge_mask[:, 0, :], op=ALU.mult)
-            if band_cols[u] == BAND:
-                nc.vector.tensor_tensor(
-                    out=ew[u][:, block(2)], in0=ew[u][:, block(2)], in1=edge_mask[:, 1, :], op=ALU.mult
-                )
+        def norm_squares(z, bias):
+            squares = work.tile([P, PIECE], BF16, name="squares")
+            nc.scalar.activation(out=squares[:], in_=z[:], func=ACT.Square, bias=bias[:, 0:1])
+            return squares
 
-        z_bias_in = held.tile([P, 2], F32, name="z_bias_in")
-        nc.vector.tensor_scalar(out=z_bias_in[:, 0:1], in0=bo_sb[:], scalar1=1.0 / SC, scalar2=None, op0=ALU.mult)
-        nc.vector.tensor_copy(z_bias_in[:, 1:2], b2_sb[:])
-        z_bias_ps = new_bank("z_bias_ps")
-        nc.tensor.matmul(z_bias_ps[:, 0:2], center_f[:], z_bias_in[:], start=True, stop=True)
-        z_bias = held.tile([P, 2], F32, name="z_bias")
-        nc.vector.tensor_copy(z_bias[:], z_bias_ps[:, 0:2])
+        def norm_rstd(squares, eps):
+            var = new_bank("var")
+            nc.tensor.matmul(var[:], mean_w[:], squares[:], start=True, stop=True)
+            rstd = work.tile([P, PIECE], F32, name="rstd")
+            nc.scalar.activation(out=rstd[:], in_=var[:], func=ACT.Abs_reciprocal_sqrt, bias=eps[:, 0:1])
+            return rstd
 
-        y = {}
+        def norm_apply(normal, z, bias, rstd):
+            scaled = work.tile([P, PIECE], F32, name="scaled")
+            nc.vector.scalar_tensor_tensor(
+                out=scaled[:], in0=z[:], scalar=bias[:, 0:1], in1=rstd[:], op0=ALU.add, op1=ALU.mult
+            )
+            nc.vector.tensor_scalar(
+                out=normal[:], in0=scaled[:], scalar1=gain[:, 0:1], scalar2=shift[:, 0:1], op0=ALU.mult, op1=ALU.add
+            )
 
-        def mix(r):
-            num = new_bank("num")
+        num, inverse, z1, squares1, n1 = {}, {}, {}, {}, {}
+
+        def mix_start(r):
+            num[r] = new_bank("num")
             den = new_bank("den")
             for b in range(BLOCKS_PER_PIECE):
                 j = r * BLOCKS_PER_PIECE + b
@@ -237,7 +246,7 @@ def tile_decoderonlyaft_b_kernel(
                     ur, ub = divmod(u, BLOCKS_PER_PIECE)
                     seen = ew[u][:, block(j - u)]
                     first, last = u == attended[0], u == attended[-1]
-                    nc.tensor.matmul(num[:, block(b)], kT[ur][:, block(2 * ub)], seen, start=first, stop=last)
+                    nc.tensor.matmul(num[r][:, block(b)], kT[ur][:, block(2 * ub)], seen, start=first, stop=last)
                     nc.tensor.matmul(den[:, block(b)], kT[ur][:, block(2 * ub + 1)], seen, start=first, stop=last)
             divisor = work.tile([P, PIECE], F32, name="divisor")
             nc.vector.scalar_tensor_tensor(
@@ -245,66 +254,86 @@ def tile_decoderonlyaft_b_kernel(
             )
             inverse_root = work.tile([P, PIECE], F32, name="inverse_root")
             nc.scalar.activation(out=inverse_root[:], in_=divisor[:], func=ACT.Abs_reciprocal_sqrt)
-            inverse = work.tile([P, PIECE], F32, name="inverse")
-            nc.scalar.activation(out=inverse[:], in_=inverse_root[:], func=ACT.Square)
-            y[r] = held.tile([P, PIECE], BF16, name="y%d" % r)
-            nc.vector.tensor_tensor(out=y[r][:], in0=num[:], in1=inverse[:], op=ALU.mult)
+            inverse[r] = work.tile([P, PIECE], F32, name="inverse")
+            nc.scalar.activation(out=inverse[r][:], in_=inverse_root[:], func=ACT.Square)
 
-        def normalise(z, bias, eps):
-            squares = work.tile([P, PIECE], BF16, name="squares")
-            nc.scalar.activation(out=squares[:], in_=z[:], func=ACT.Square, bias=bias)
-            var = new_bank("var")
-            nc.tensor.matmul(var[:], mean_w[:], squares[:], start=True, stop=True)
-            rstd = work.tile([P, PIECE], F32, name="rstd")
-            nc.scalar.activation(out=rstd[:], in_=var[:], func=ACT.Abs_reciprocal_sqrt, bias=eps[:, 0:1])
-            normed = work.tile([P, PIECE], F32, name="normed")
-            nc.vector.scalar_tensor_tensor(
-                out=normed[:], in0=z[:], scalar=bias, in1=rstd[:], op0=ALU.add, op1=ALU.mult
-            )
-            return normed
+        def mix_end(r):
+            y = work.tile([P, PIECE], BF16, name="y")
+            nc.vector.tensor_tensor(out=y[:], in0=num[r][:], in1=inverse[r][:], op=ALU.mult)
+            z1[r] = new_bank("z1")
+            nc.tensor.matmul(z1[r][:], center[:], words[r][:], start=True, stop=False)
+            nc.tensor.matmul(z1[r][:], center2[:], pos_sb[:, piece(r)], start=False, stop=False)
+            nc.tensor.matmul(z1[r][:], wo_c[:], y[:], start=False, stop=True)
+            squares1[r] = norm_squares(z1[r], z1_bias)
 
-        n1 = {}
-
-        def first_norm(r):
-            z1 = new_bank("z1")
-            nc.tensor.matmul(z1[:], center[:], words[r][:], start=True, stop=False)
-            nc.tensor.matmul(z1[:], center2[:], pos_sb[:, piece(r)], start=False, stop=False)
-            nc.tensor.matmul(z1[:], wo_c[:], y[r][:], start=False, stop=True)
-            normed1 = normalise(z1, z_bias[:, 0:1], eps1)
+        def norm_end(r):
             n1[r] = held.tile([P, PIECE], BF16, name="n1_%d" % r)
-            nc.vector.tensor_scalar(
-                out=n1[r][:], in0=normed1[:], scalar1=gain[:, 0:1], scalar2=shift[:, 0:1], op0=ALU.mult, op1=ALU.add
-            )
+            norm_apply(n1[r], z1[r], z1_bias, norm_rstd(squares1[r], eps1))
 
-        def feed_forward(r):
-            z2 = new_bank("z2")
-            nc.tensor.matmul(z2[:], center[:], n1[r][:], start=True, stop=False)
-            hid = {}
-            for a in range(HID_BLOCKS + AHEAD):
-                if a < HID_BLOCKS:
-                    hid_ps = new_bank("hid_ps")
-                    nc.tensor.matmul(hid_ps[:], w1_sb[:, block(a)], n1[r][:], start=True, stop=True)
-                    hid[a] = hidden.tile([P, PIECE], BF16, name="hid")
-                    if a % 3 == 0:
-                        nc.scalar.activation(out=hid[a][:], in_=hid_ps[:], func=ACT.Relu, bias=b1_sb[:, a : a + 1])
-                    else:
-                        nc.vector.tensor_scalar(
-                            out=hid[a][:], in0=hid_ps[:], scalar1=b1_sb[:, a : a + 1], scalar2=0.0,
-                            op0=ALU.add, op1=ALU.max,
-                        )
-                if a >= AHEAD:
-                    done = a - AHEAD
-                    nc.tensor.matmul(z2[:], w2_c[:, done, :], hid[done][:], start=False, stop=(done == HID_BLOCKS - 1))
-            normed2 = normalise(z2, z_bias[:, 1:2], eps2)
-            result = work.tile([P, PIECE], F32, name="result")
-            nc.vector.tensor_scalar(
-                out=result[:], in0=normed2[:], scalar1=gain[:, 0:1], scalar2=shift[:, 0:1], op0=ALU.mult, op1=ALU.add
-            )
-            nc.sync.dma_start(out[:, piece(r)], result[:])
+        def centred(vec, name):
+            vec_ps = new_bank("vec_ps")
+            nc.tensor.matmul(vec_ps[:, 0:1], center_f[:], vec[:], start=True, stop=True)
+            t = held.tile([P, 1], F32, name=name)
+            nc.vector.tensor_copy(t[:], vec_ps[:, 0:1])
+            return t
 
-        for r in range(N_PIECES + 2):
+        mix_start(0)
+        flip(2)
+        mix_start(1)
+        flip(3)
+        wo_sum = held.tile([P, 1], F32, name="wo_sum")
+        nc.vector.tensor_reduce(out=wo_sum[:], in_=wo_sb[:], axis=mybir.AxisListType.X, op=ALU.add)
+        wo_mean = held.tile([P, 1], F32, name="wo_mean")
+        nc.vector.tensor_scalar(out=wo_mean[:], in0=wo_sum[:], scalar1=1.0 / P, scalar2=None, op0=ALU.mult)
+        wo_c = held.tile([P, P], BF16, name="wo_c")
+        nc.vector.tensor_scalar(out=wo_c[:], in0=wo_sb[:], scalar1=wo_mean[:, 0:1], scalar2=None, op0=ALU.subtract)
+        bo_over_sc = held.tile([P, 1], F32, name="bo_over_sc")
+        nc.vector.tensor_scalar(out=bo_over_sc[:], in0=bo_sb[:], scalar1=1.0 / SC, scalar2=None, op0=ALU.mult)
+        z1_bias = centred(bo_over_sc, "z1_bias")
+        z2_bias = centred(b2_sb, "z2_bias")
+        for r in range(2, N_PIECES + 4):
             if r < N_PIECES:
-                mix(r)
-                first_norm(r)
-            if r >= 2:
-                feed_forward(r - 2)
+                mix_start(r)
+            if r - 2 < N_PIECES:
+                mix_end(r - 2)
+            if r >= 4:
+                norm_end(r - 4)
+
+        z2, squares2, rstd2 = {}, {}, {}
+
+        def second_norm_step(r, step):
+            if step == 0:
+                squares2[r] = norm_squares(z2[r], z2_bias)
+            elif step == 1:
+                rstd2[r] = norm_rstd(squares2[r], eps2)
+            else:
+                result = work.tile([P, PIECE], F32, name="result")
+                norm_apply(result, z2[r], z2_bias, rstd2[r])
+                nc.sync.dma_start(out[:, piece(r)], result[:])
+
+        hid = {}
+        for g in range(N_PIECES * HID_BLOCKS + AHEAD):
+            r, a = divmod(g, HID_BLOCKS)
+            if r < N_PIECES:
+                if a == 0:
+                    z2[r] = new_bank("z2")
+                    nc.tensor.matmul(z2[r][:], center[:], n1[r][:], start=True, stop=False)
+                hid_ps = new_bank("hid_ps")
+                nc.tensor.matmul(hid_ps[:], w1_sb[:, block(a)], n1[r][:], start=True, stop=True)
+                hid[g] = hidden.tile([P, PIECE], BF16, name="hid")
+                if a % 3 == 0:
+                    nc.scalar.activation(out=hid[g][:], in_=hid_ps[:], func=ACT.Relu, bias=b1_sb[:, a : a + 1])
+                else:
+                    nc.vector.tensor_scalar(
+                        out=hid[g][:], in0=hid_ps[:], scalar1=b1_sb[:, a : a + 1], scalar2=0.0,
+                        op0=ALU.add, op1=ALU.max,
+                    )
+            if g >= AHEAD:
+                done_r, done_a = divmod(g - AHEAD, HID_BLOCKS)
+                nc.tensor.matmul(
+                    z2[done_r][:], w2_c[:, done_a, :], hid[g - AHEAD][:], start=False, stop=(done_a == HID_BLOCKS - 1)
+                )
+            if 0 < r < N_PIECES and a in (AHEAD, AHEAD + 2, AHEAD + 4):
+                second_norm_step(r - 1, (a - AHEAD) // 2)
+        for step in range(3):
+            second_norm_step(N_PIECES - 1, step)

@@ -42,7 +42,6 @@ def tile_decoderonlyaft_b_kernel(
 ):
     nc = tc.nc
     with ExitStack() as ctx:
-        ctx.enter_context(nc.allow_non_contiguous_dma(reason="b1 is loaded one value to a partition"))
         held = ctx.enter_context(tc.tile_pool(name="held", bufs=1))
         work = ctx.enter_context(tc.tile_pool(name="work", bufs=4))
         hidden = ctx.enter_context(tc.tile_pool(name="hidden", bufs=6))
@@ -81,11 +80,11 @@ def tile_decoderonlyaft_b_kernel(
         bv_sb = load(nc.scalar, [P, 1], F32, "bv_sb", bv)
         bq_sb = load(nc.gpsimd, [P, 1], F32, "bq_sb", bq)
         wb = [load_band(nc.scalar if m % 2 == 0 else nc.sync, m) for m in range(BLOCKS // 2)]
-        w2_sb = load(nc.gpsimd, [P, HID_BLOCKS, P], BF16, "w2_sb", w2.rearrange("(a p) c -> p a c", p=P))
+        w2_sb = load(nc.gpsimd, [P, HID_BLOCKS, P], BF16, "w2_sb", w2.rearrange("(p a) c -> p a c", a=HID_BLOCKS))
         bo_sb = load(nc.gpsimd, [P, 1], F32, "bo_sb", bo)
         wo_sb = load(nc.sync, [P, P], BF16, "wo_sb", wo)
         gain = load(nc.scalar, [P, 1], F32, "gain", ln_gain)
-        b1_sb = load(nc.gpsimd, [P, HID_BLOCKS], F32, "b1_sb", b1.rearrange("(a p) o -> p (a o)", p=P))
+        b1_sb = load(nc.gpsimd, [P, HID_BLOCKS], F32, "b1_sb", b1.rearrange("(p a) o -> p (a o)", a=HID_BLOCKS))
         w1_sb = load(nc.sync, [P, HID], BF16, "w1_sb", w1)
         shift = load(nc.scalar, [P, 1], F32, "shift", ln_shift)
         b2_sb = load(nc.gpsimd, [P, 1], F32, "b2_sb", b2)
@@ -319,7 +318,7 @@ def tile_decoderonlyaft_b_kernel(
                     z2[r] = new_bank("z2")
                     nc.tensor.matmul(z2[r][:], center[:], n1[r][:], start=True, stop=False)
                 hid_ps = new_bank("hid_ps")
-                nc.tensor.matmul(hid_ps[:], w1_sb[:, block(a)], n1[r][:], start=True, stop=True)
+                nc.tensor.matmul(hid_ps[:], w1_sb[:, a : HID : HID_BLOCKS], n1[r][:], start=True, stop=True)
                 hid[g] = hidden.tile([P, PIECE], BF16, name="hid")
                 if a % 3 == 0:
                     nc.scalar.activation(out=hid[g][:], in_=hid_ps[:], func=ACT.Relu, bias=b1_sb[:, a : a + 1])

@@ -25,7 +25,6 @@ BAND = WIN + P
 HID_BLOCKS = HID // P
 KEY, VAL, QRY = 0, 1, 2
 AHEAD = 4
-EARLY_BAND_BLOCKS = 12
 
 FLOPS = 2 * P * P * N * 4 + 2 * 2 * P * WIN * N + 2 * 2 * P * HID * N
 BYTES = (
@@ -61,42 +60,8 @@ def tile_decoderonlyaft_b_kernel(
             queue.dma_start(t[:], source)
             return t
 
-        def load_band(queue, m):
-            first = 2 * P * m
-            cols = min(4 * P, N - first)
-            source = wbias[first : first + 2 * P, first : first + cols].rearrange("(a p) x -> p a x", p=P)
-            return load(queue, [P, 2, cols], F32, "wb%d" % m, source)
-
-        w_sb = {}
-        pos_sb = load(nc.sync, [P, N], BF16, "pos_sb", pos)
-        w_sb[KEY] = load(nc.scalar, [P, P], BF16, "wk_sb", wk)
-        w_sb[VAL] = load(nc.gpsimd, [P, P], BF16, "wv_sb", wv)
-        offsets = held.tile([P, N // 16], U16, name="offsets")
-        nc.sync.dma_start(offsets[:], offs)
-        w_sb[QRY] = load(nc.scalar, [P, P], BF16, "wq_sb", wq)
-        table_sb = load(nc.gpsimd, [P, S], BF16, "table_sb", table)
-        ident = held.tile([P, P], BF16, name="ident")
-        make_identity(nc, ident[:])
-        bv_sb = load(nc.scalar, [P, 1], F32, "bv_sb", bv)
-        bq_sb = load(nc.gpsimd, [P, 1], F32, "bq_sb", bq)
-        wb = [load_band(nc.scalar if m % 2 == 0 else nc.sync, m) for m in range(BLOCKS // 2)]
-        w2_sb = load(nc.gpsimd, [P, HID_BLOCKS, P], BF16, "w2_sb", w2.rearrange("(p a) c -> p a c", a=HID_BLOCKS))
-        bo_sb = load(nc.gpsimd, [P, 1], F32, "bo_sb", bo)
-        wo_sb = load(nc.sync, [P, P], BF16, "wo_sb", wo)
-        gain = load(nc.scalar, [P, 1], F32, "gain", ln_gain)
-        b1_sb = load(nc.gpsimd, [P, HID_BLOCKS], F32, "b1_sb", b1.rearrange("(p a) o -> p (a o)", a=HID_BLOCKS))
-        w1_sb = load(nc.sync, [P, HID], BF16, "w1_sb", w1)
-        shift = load(nc.scalar, [P, 1], F32, "shift", ln_shift)
-        b2_sb = load(nc.gpsimd, [P, 1], F32, "b2_sb", b2)
-
-        w_twice = {}
-        for which in (KEY, VAL, QRY):
-            w_twice[which] = held.tile([P, P], BF16, name="w_twice%d" % which)
-            nc.vector.tensor_scalar(out=w_twice[which][:], in0=w_sb[which][:], scalar1=2.0, scalar2=None, op0=ALU.mult)
-        bv_over_sc = held.tile([P, 1], F32, name="bv_over_sc")
-        nc.vector.tensor_scalar(out=bv_over_sc[:], in0=bv_sb[:], scalar1=1.0 / SC, scalar2=None, op0=ALU.mult)
-        neg_bq = held.tile([P, 1], F32, name="neg_bq")
-        nc.vector.tensor_scalar(out=neg_bq[:], in0=bq_sb[:], scalar1=-1.0, scalar2=None, op0=ALU.mult)
+        w_sb, wb = {}, {}
+        w_sb[QRY] = load(nc.gpsimd, [P, P], BF16, "wq_sb", wq)
 
         edge_mask = held.tile([P, 2, P], BF16, name="edge_mask")
         nc.gpsimd.memset(edge_mask[:], 1.0)
@@ -108,81 +73,50 @@ def tile_decoderonlyaft_b_kernel(
             out=edge_mask[:, 1, :], in_=edge_mask[:, 1, :], compare_op=ALU.is_gt, fill=0.0,
             base=0, pattern=[[-1, P]], channel_multiplier=1,
         )
+        ident = held.tile([P, P], BF16, name="ident")
+        make_identity(nc, ident[:])
         ident_f = held.tile([P, P], F32, name="ident_f")
         make_identity(nc, ident_f[:])
 
-        def project_pos(bank, which, r, start, stop):
-            nc.tensor.matmul(bank[:], w_twice[which][:], pos_sb[:, piece(r)], start=start, stop=stop)
+        wbias_flat = wbias.rearrange("u j -> (u j)")
+        window_step = P * (N + 1)
 
-        def project_table(bank, weights, r, start, stop):
-            looked_up = table_sb[:].indirect(offsets[:, r * OFFS_COLS : (r + 1) * OFFS_COLS])
-            nc.tensor.matmul(bank[:], weights, looked_up, start=start, stop=stop)
+        def load_band(queue, m):
+            if m == BLOCKS // 2 - 1:
+                source = wbias[N - 2 * P : N, N - 2 * P : N].rearrange("(a p) x -> p a x", p=P)
+                return load(queue, [P, 2, 2 * P], F32, "wb%d" % m, source)
+            two = wbias_flat[2 * m * window_step : (2 * m + 2) * window_step].rearrange("(a r) -> a r", r=window_step)
+            source = two[:, 0 : P * N].rearrange("a (p j) -> p a j", j=N)[:, :, 0:BAND]
+            return load(queue, [P, 2, BAND], F32, "wb%d" % m, source)
 
-        ek, ekv, eq, words = {}, {}, {}, {}
+        pos_sb = load(nc.sync, [P, N], BF16, "pos_sb", pos)
+        w_sb[KEY] = load(nc.scalar, [P, P], BF16, "wk_sb", wk)
+        wb[0] = load_band(nc.sync, 0)
+        w_sb[VAL] = load(nc.scalar, [P, P], BF16, "wv_sb", wv)
+        offsets = held.tile([P, N // 16], U16, name="offsets")
+        nc.sync.dma_start(offsets[:], offs)
+        wb[1] = load_band(nc.scalar, 1)
+        table_sb = load(nc.sync, [P, S], BF16, "table_sb", table)
+        bv_sb = load(nc.sync, [P, 1], F32, "bv_sb", bv)
+        wb[2] = load_band(nc.sync, 2)
+        bq_sb = load(nc.sync, [P, 1], F32, "bq_sb", bq)
+        wb[3] = load_band(nc.sync, 3)
+        wb[4] = load_band(nc.sync, 4)
+        bo_sb = load(nc.sync, [P, 1], F32, "bo_sb", bo)
+        for m in range(5, BLOCKS // 2):
+            wb[m] = load_band(nc.sync, m)
+        wo_sb = load(nc.sync, [P, P], BF16, "wo_sb", wo)
+        w1_sb = load(nc.sync, [P, HID], BF16, "w1_sb", w1)
+        w2_sb = load(nc.sync, [P, HID_BLOCKS, P], BF16, "w2_sb", w2.rearrange("(p a) c -> p a c", a=HID_BLOCKS))
+        b2_sb = load(nc.gpsimd, [P, 1], F32, "b2_sb", b2)
+        gain = load(nc.gpsimd, [P, 1], F32, "gain", ln_gain)
+        shift = load(nc.gpsimd, [P, 1], F32, "shift", ln_shift)
+        b1_sb = load(nc.gpsimd, [P, HID_BLOCKS], F32, "b1_sb", b1.rearrange("(p a) o -> p (a o)", a=HID_BLOCKS))
 
-        def finish(bank, which, r):
-            if which == KEY:
-                ek[r] = work.tile([P, PIECE], BF16, name="ek")
-                nc.scalar.activation(out=ek[r][:], in_=bank[:], func=ACT.Exp, scale=SC)
-            elif which == VAL:
-                ekv[r] = work.tile([P, PIECE], BF16, name="ekv")
-                nc.vector.scalar_tensor_tensor(
-                    out=ekv[r][:], in0=bank[:], scalar=bv_over_sc[:, 0:1], in1=ek[r][:], op0=ALU.add, op1=ALU.mult
-                )
-            else:
-                eq[r] = held.tile([P, PIECE], F32, name="eq%d" % r)
-                nc.scalar.activation(out=eq[r][:], in_=bank[:], func=ACT.Exp, scale=-SC, bias=neg_bq[:, 0:1])
-
-        kT = {}
-
-        def flip(r):
-            flipped = psum.tile([P, 2 * PIECE], BF16, name="flipped", tag="bank")
-            for b in range(BLOCKS_PER_PIECE):
-                nc.tensor.transpose(flipped[:, block(2 * b)], ekv[r][:, block(b)], ident[:])
-                nc.tensor.transpose(flipped[:, block(2 * b + 1)], ek[r][:, block(b)], ident[:])
-            kT[r] = held.tile([P, 2 * PIECE], BF16, name="kT%d" % r)
-            nc.vector.tensor_copy(kT[r][:], flipped[:])
-
-        band_cols = [min(BAND, N - P * u) for u in range(BLOCKS)]
-        ew = {}
-
-        def band_weights(u):
-            m, a = divmod(u, 2)
-            ew[u] = held.tile([P, band_cols[u]], BF16, name="ew%d" % u)
-            nc.scalar.activation(out=ew[u][:], in_=wb[m][:, a, a * P : a * P + band_cols[u]], func=ACT.Exp)
-            nc.vector.tensor_tensor(out=ew[u][:, block(0)], in0=ew[u][:, block(0)], in1=edge_mask[:, 0, :], op=ALU.mult)
-            if band_cols[u] == BAND:
-                nc.vector.tensor_tensor(
-                    out=ew[u][:, block(2)], in0=ew[u][:, block(2)], in1=edge_mask[:, 1, :], op=ALU.mult
-                )
-
-        order = ((KEY, VAL), (QRY,))
-        banks = {}
-        for group in order:
-            for r in (0, 1):
-                for which in group:
-                    banks[r, which] = new_bank("proj")
-                    project_pos(banks[r, which], which, r, start=True, stop=False)
-        for group in order:
-            for r in (0, 1):
-                for which in group:
-                    project_table(banks[r, which], w_sb[which][:], r, start=False, stop=True)
-                    finish(banks[r, which], which, r)
-        for r in range(N_PIECES):
-            words_ps = new_bank("words_ps")
-            project_table(words_ps, ident[:], r, start=True, stop=True)
-            words[r] = held.tile([P, PIECE], BF16, name="words%d" % r)
-            nc.vector.tensor_copy(words[r][:], words_ps[:])
-        flip(0)
-        flip(1)
-        for group in order:
-            for r in (2, 3):
-                for which in group:
-                    banks[r, which] = new_bank("proj")
-                    project_table(banks[r, which], w_sb[which][:], r, start=True, stop=False)
-
-        for u in range(EARLY_BAND_BLOCKS):
-            band_weights(u)
+        w_twice = {}
+        for which in (KEY, VAL, QRY):
+            w_twice[which] = held.tile([P, P], BF16, name="w_twice%d" % which)
+            nc.vector.tensor_scalar(out=w_twice[which][:], in0=w_sb[which][:], scalar1=2.0, scalar2=None, op0=ALU.mult)
         center_f = held.tile([P, P], F32, name="center_f")
         nc.vector.tensor_scalar(out=center_f[:], in0=ident_f[:], scalar1=-1.0 / P, scalar2=None, op0=ALU.add)
         center = held.tile([P, P], BF16, name="center")
@@ -195,91 +129,72 @@ def tile_decoderonlyaft_b_kernel(
         nc.vector.memset(eps1[:], EPS / (SC * SC))
         eps2 = held.tile([P, 1], F32, name="eps2")
         nc.vector.memset(eps2[:], EPS)
-        w2_sum = held.tile([P, HID_BLOCKS], F32, name="w2_sum")
-        nc.vector.tensor_reduce(out=w2_sum[:], in_=w2_sb[:], axis=mybir.AxisListType.X, op=ALU.add)
-        w2_negmean = held.tile([P, HID_BLOCKS], F32, name="w2_negmean")
-        nc.vector.tensor_scalar(out=w2_negmean[:], in0=w2_sum[:], scalar1=-1.0 / P, scalar2=None, op0=ALU.mult)
-        w2_c = held.tile([P, HID_BLOCKS, P], BF16, name="w2_c")
-        nc.gpsimd.tensor_tensor(
-            out=w2_c[:], in0=w2_sb[:], in1=w2_negmean[:].unsqueeze(2).to_broadcast([P, HID_BLOCKS, P]), op=ALU.add
-        )
 
-        for group in order:
-            for r in (2, 3):
-                for which in group:
-                    project_pos(banks[r, which], which, r, start=False, stop=True)
-                    finish(banks[r, which], which, r)
-        for u in range(EARLY_BAND_BLOCKS, BLOCKS):
+        def project_pos(bank, weights, r, start, stop):
+            nc.tensor.matmul(bank[:], weights, pos_sb[:, piece(r)], start=start, stop=stop)
+
+        def project_table(bank, weights, r, start, stop):
+            looked_up = table_sb[:].indirect(offsets[:, r * OFFS_COLS : (r + 1) * OFFS_COLS])
+            nc.tensor.matmul(bank[:], weights, looked_up, start=start, stop=stop)
+
+        bv_over_sc = held.tile([P, 1], F32, name="bv_over_sc")
+        neg_bq = held.tile([P, 1], F32, name="neg_bq")
+        banks, ek, ekv, eq = {}, {}, {}, {}
+
+        def finish(r, which):
+            if which == KEY:
+                ek[r] = work.tile([P, PIECE], BF16, name="ek")
+                nc.scalar.activation(out=ek[r][:], in_=banks[r, which][:], func=ACT.Exp, scale=SC)
+            elif which == VAL:
+                ekv[r] = work.tile([P, PIECE], BF16, name="ekv")
+                nc.vector.scalar_tensor_tensor(
+                    out=ekv[r][:], in0=banks[r, which][:], scalar=bv_over_sc[:, 0:1], in1=ek[r][:],
+                    op0=ALU.add, op1=ALU.mult,
+                )
+            else:
+                eq[r] = held.tile([P, PIECE], F32, name="eq%d" % r)
+                nc.scalar.activation(
+                    out=eq[r][:], in_=banks[r, which][:], func=ACT.Exp, scale=-SC, bias=neg_bq[:, 0:1]
+                )
+
+        ew = {}
+
+        def band_weights(u):
+            m, a = divmod(u, 2)
+            seen_blocks = min(BAND, N - P * u) // P
+            first = a * P if m == BLOCKS // 2 - 1 else 0
+            ew[u] = held.tile([P, seen_blocks * P], BF16, name="ew%d" % u)
+            nc.scalar.activation(out=ew[u][:], in_=wb[m][:, a, first : first + seen_blocks * P], func=ACT.Exp)
+            if seen_blocks == 3:
+                edges = ew[u][:].rearrange("p (b x) -> p b x", x=P)[:, 0:3:2, :]
+                nc.vector.tensor_tensor(out=edges, in0=edges, in1=edge_mask[:], op=ALU.mult)
+            else:
+                nc.vector.tensor_tensor(out=ew[u][:, block(0)], in0=ew[u][:, block(0)], in1=edge_mask[:, 0, :], op=ALU.mult)
+
+        first_run = ((0, KEY), (0, VAL), (1, KEY), (2, KEY), (3, KEY), (0, QRY), (1, QRY), (2, QRY))
+        second_run = ((1, VAL), (2, VAL), (3, VAL))
+
+        def open_by_pos(r, which):
+            banks[r, which] = new_bank("proj")
+            project_pos(banks[r, which], w_twice[which][:], r, start=True, stop=False)
+
+        def close_by_table(r, which):
+            project_table(banks[r, which], w_sb[which][:], r, start=False, stop=True)
+            finish(r, which)
+
+        for r, which in first_run:
+            open_by_pos(r, which)
+        nc.vector.tensor_scalar(out=bv_over_sc[:], in0=bv_sb[:], scalar1=1.0 / SC, scalar2=None, op0=ALU.mult)
+        nc.vector.tensor_scalar(out=neg_bq[:], in0=bq_sb[:], scalar1=-1.0, scalar2=None, op0=ALU.mult)
+        for r, which in first_run:
+            close_by_table(r, which)
+        banks[3, QRY] = new_bank("proj")
+        project_table(banks[3, QRY], w_sb[QRY][:], 3, start=True, stop=False)
+        project_pos(banks[3, QRY], w_twice[QRY][:], 3, start=False, stop=True)
+        finish(3, QRY)
+        for u in range(BLOCKS):
             band_weights(u)
 
-        def norm_squares(z, bias):
-            squares = work.tile([P, PIECE], BF16, name="squares")
-            nc.scalar.activation(out=squares[:], in_=z[:], func=ACT.Square, bias=bias[:, 0:1])
-            return squares
-
-        def norm_rstd(squares, eps):
-            var = new_bank("var")
-            nc.tensor.matmul(var[:], mean_w[:], squares[:], start=True, stop=True)
-            rstd = work.tile([P, PIECE], F32, name="rstd")
-            nc.scalar.activation(out=rstd[:], in_=var[:], func=ACT.Abs_reciprocal_sqrt, bias=eps[:, 0:1])
-            return rstd
-
-        def norm_apply(normal, z, bias, rstd):
-            scaled = work.tile([P, PIECE], F32, name="scaled")
-            nc.vector.scalar_tensor_tensor(
-                out=scaled[:], in0=z[:], scalar=bias[:, 0:1], in1=rstd[:], op0=ALU.add, op1=ALU.mult
-            )
-            nc.vector.tensor_scalar(
-                out=normal[:], in0=scaled[:], scalar1=gain[:, 0:1], scalar2=shift[:, 0:1], op0=ALU.mult, op1=ALU.add
-            )
-
-        num, inverse, z1, squares1, n1 = {}, {}, {}, {}, {}
-
-        def mix_start(r):
-            num[r] = new_bank("num")
-            den = new_bank("den")
-            for b in range(BLOCKS_PER_PIECE):
-                j = r * BLOCKS_PER_PIECE + b
-                attended = [u for u in (j - 2, j - 1, j) if u >= 0]
-                for u in attended:
-                    ur, ub = divmod(u, BLOCKS_PER_PIECE)
-                    seen = ew[u][:, block(j - u)]
-                    first, last = u == attended[0], u == attended[-1]
-                    nc.tensor.matmul(num[r][:, block(b)], kT[ur][:, block(2 * ub)], seen, start=first, stop=last)
-                    nc.tensor.matmul(den[:, block(b)], kT[ur][:, block(2 * ub + 1)], seen, start=first, stop=last)
-            divisor = work.tile([P, PIECE], F32, name="divisor")
-            nc.vector.scalar_tensor_tensor(
-                out=divisor[:], in0=eq[r][:], scalar=1.0, in1=den[:], op0=ALU.add, op1=ALU.mult
-            )
-            inverse_root = work.tile([P, PIECE], F32, name="inverse_root")
-            nc.scalar.activation(out=inverse_root[:], in_=divisor[:], func=ACT.Abs_reciprocal_sqrt)
-            inverse[r] = work.tile([P, PIECE], F32, name="inverse")
-            nc.scalar.activation(out=inverse[r][:], in_=inverse_root[:], func=ACT.Square)
-
-        def mix_end(r):
-            y = work.tile([P, PIECE], BF16, name="y")
-            nc.vector.tensor_tensor(out=y[:], in0=num[r][:], in1=inverse[r][:], op=ALU.mult)
-            z1[r] = new_bank("z1")
-            nc.tensor.matmul(z1[r][:], center[:], words[r][:], start=True, stop=False)
-            nc.tensor.matmul(z1[r][:], center2[:], pos_sb[:, piece(r)], start=False, stop=False)
-            nc.tensor.matmul(z1[r][:], wo_c[:], y[:], start=False, stop=True)
-            squares1[r] = norm_squares(z1[r], z1_bias)
-
-        def norm_end(r):
-            n1[r] = held.tile([P, PIECE], BF16, name="n1_%d" % r)
-            norm_apply(n1[r], z1[r], z1_bias, norm_rstd(squares1[r], eps1))
-
-        def centred(vec, name):
-            vec_ps = new_bank("vec_ps")
-            nc.tensor.matmul(vec_ps[:, 0:1], center_f[:], vec[:], start=True, stop=True)
-            t = held.tile([P, 1], F32, name=name)
-            nc.vector.tensor_copy(t[:], vec_ps[:, 0:1])
-            return t
-
-        mix_start(0)
-        flip(2)
-        mix_start(1)
-        flip(3)
         wo_sum = held.tile([P, 1], F32, name="wo_sum")
         nc.vector.tensor_reduce(out=wo_sum[:], in_=wo_sb[:], axis=mybir.AxisListType.X, op=ALU.add)
         wo_mean = held.tile([P, 1], F32, name="wo_mean")
@@ -288,30 +203,137 @@ def tile_decoderonlyaft_b_kernel(
         nc.vector.tensor_scalar(out=wo_c[:], in0=wo_sb[:], scalar1=wo_mean[:, 0:1], scalar2=None, op0=ALU.subtract)
         bo_over_sc = held.tile([P, 1], F32, name="bo_over_sc")
         nc.vector.tensor_scalar(out=bo_over_sc[:], in0=bo_sb[:], scalar1=1.0 / SC, scalar2=None, op0=ALU.mult)
-        z1_bias = centred(bo_over_sc, "z1_bias")
-        z2_bias = centred(b2_sb, "z2_bias")
-        for r in range(2, N_PIECES + 4):
-            if r < N_PIECES:
-                mix_start(r)
-            if r - 2 < N_PIECES:
-                mix_end(r - 2)
-            if r >= 4:
-                norm_end(r - 4)
 
-        z2, squares2, rstd2 = {}, {}, {}
+        kT, num, den, divisor, inverse_root, inverse, y, z1, n1 = {}, {}, {}, {}, {}, {}, {}, {}, {}
 
-        def second_norm_step(r, step):
-            if step == 0:
-                squares2[r] = norm_squares(z2[r], z2_bias)
-            elif step == 1:
-                rstd2[r] = norm_rstd(squares2[r], eps2)
-            else:
-                result = work.tile([P, PIECE], F32, name="result")
-                norm_apply(result, z2[r], z2_bias, rstd2[r])
-                nc.sync.dma_start(out[:, piece(r)], result[:])
+        def flip(r):
+            flipped = psum.tile([P, 2 * PIECE], BF16, name="flipped", tag="bank")
+            for b in range(BLOCKS_PER_PIECE):
+                nc.tensor.transpose(flipped[:, block(2 * b)], ekv[r][:, block(b)], ident[:])
+                nc.tensor.transpose(flipped[:, block(2 * b + 1)], ek[r][:, block(b)], ident[:])
+            kT[r] = held.tile([P, 2 * PIECE], BF16, name="kT%d" % r)
+            nc.vector.tensor_copy(kT[r][:], flipped[:])
 
-        hid = {}
-        for g in range(N_PIECES * HID_BLOCKS + AHEAD):
+        def sums(r):
+            num[r] = new_bank("num")
+            den[r] = new_bank("den")
+            for b in range(BLOCKS_PER_PIECE):
+                j = r * BLOCKS_PER_PIECE + b
+                attended = [u for u in (j - 2, j - 1, j) if u >= 0]
+                for u in attended:
+                    ur, ub = divmod(u, BLOCKS_PER_PIECE)
+                    seen = ew[u][:, block(j - u)]
+                    first, last = u == attended[0], u == attended[-1]
+                    nc.tensor.matmul(num[r][:, block(b)], kT[ur][:, block(2 * ub)], seen, start=first, stop=last)
+                    nc.tensor.matmul(den[r][:, block(b)], kT[ur][:, block(2 * ub + 1)], seen, start=first, stop=last)
+
+        def divide_1(r):
+            divisor[r] = work.tile([P, PIECE], F32, name="divisor")
+            nc.vector.scalar_tensor_tensor(
+                out=divisor[r][:], in0=eq[r][:], scalar=1.0, in1=den[r][:], op0=ALU.add, op1=ALU.mult
+            )
+
+        def divide_2(r):
+            inverse_root[r] = work.tile([P, PIECE], F32, name="inverse_root")
+            nc.scalar.activation(out=inverse_root[r][:], in_=divisor[r][:], func=ACT.Abs_reciprocal_sqrt)
+
+        def divide_3(r):
+            inverse[r] = work.tile([P, PIECE], F32, name="inverse")
+            nc.scalar.activation(out=inverse[r][:], in_=inverse_root[r][:], func=ACT.Square)
+
+        def divide_4(r):
+            y[r] = work.tile([P, PIECE], BF16, name="y")
+            nc.vector.tensor_tensor(out=y[r][:], in0=num[r][:], in1=inverse[r][:], op=ALU.mult)
+
+        def residual_pos(r):
+            z1[r] = new_bank("z1")
+            project_pos(z1[r], center2[:], r, start=True, stop=False)
+
+        def residual_table(r):
+            project_table(z1[r], center[:], r, start=False, stop=False)
+
+        def residual(r):
+            residual_pos(r)
+            residual_table(r)
+
+        def project_out(r):
+            nc.tensor.matmul(z1[r][:], wo_c[:], y[r][:], start=False, stop=True)
+
+        squares, var, rstd, scaled = {}, {}, {}, {}
+
+        def norm_1(which_norm, r, z, bias):
+            squares[which_norm, r] = work.tile([P, PIECE], BF16, name="squares")
+            nc.scalar.activation(out=squares[which_norm, r][:], in_=z[:], func=ACT.Square, bias=bias[:, 0:1])
+
+        def norm_2(which_norm, r):
+            var[which_norm, r] = new_bank("var")
+            nc.tensor.matmul(var[which_norm, r][:], mean_w[:], squares[which_norm, r][:], start=True, stop=True)
+
+        def norm_3(which_norm, r, eps):
+            rstd[which_norm, r] = work.tile([P, PIECE], F32, name="rstd")
+            nc.scalar.activation(
+                out=rstd[which_norm, r][:], in_=var[which_norm, r][:], func=ACT.Abs_reciprocal_sqrt, bias=eps[:, 0:1]
+            )
+
+        def norm_4(which_norm, r, z, bias):
+            scaled[which_norm, r] = work.tile([P, PIECE], F32, name="scaled")
+            nc.vector.scalar_tensor_tensor(
+                out=scaled[which_norm, r][:], in0=z[:], scalar=bias[:, 0:1], in1=rstd[which_norm, r][:],
+                op0=ALU.add, op1=ALU.mult,
+            )
+
+        def norm_5(which_norm, r, normal):
+            nc.vector.tensor_scalar(
+                out=normal[:], in0=scaled[which_norm, r][:], scalar1=gain[:, 0:1], scalar2=shift[:, 0:1],
+                op0=ALU.mult, op1=ALU.add,
+            )
+
+        def first_norm_1(r):
+            norm_1(1, r, z1[r], z1_bias)
+
+        def first_norm_2(r):
+            norm_2(1, r)
+
+        def first_norm_3(r):
+            norm_3(1, r, eps1)
+
+        def first_norm_4(r):
+            norm_4(1, r, z1[r], z1_bias)
+
+        def first_norm_5(r):
+            n1[r] = held.tile([P, PIECE], BF16, name="n1_%d" % r)
+            norm_5(1, r, n1[r])
+
+        z2, hid = {}, {}
+
+        def second_norm_1(r):
+            norm_1(2, r, z2[r], z2_bias)
+
+        def second_norm_2(r):
+            norm_2(2, r)
+
+        def second_norm_3(r):
+            norm_3(2, r, eps2)
+
+        def second_norm_4(r):
+            norm_4(2, r, z2[r], z2_bias)
+
+        def second_norm_5(r):
+            result = work.tile([P, PIECE], F32, name="result")
+            norm_5(2, r, result)
+            nc.sync.dma_start(out[:, piece(r)], result[:])
+
+        def pause(r):
+            pass
+
+        def centred(vec, name):
+            vec_ps = new_bank("vec_ps")
+            nc.tensor.matmul(vec_ps[:, 0:1], center_f[:], vec[:], start=True, stop=True)
+            t = held.tile([P, 1], F32, name=name)
+            nc.vector.tensor_copy(t[:], vec_ps[:, 0:1])
+            return t
+
+        def hidden_block(g):
             r, a = divmod(g, HID_BLOCKS)
             if r < N_PIECES:
                 if a == 0:
@@ -332,7 +354,66 @@ def tile_decoderonlyaft_b_kernel(
                 nc.tensor.matmul(
                     z2[done_r][:], w2_c[:, done_a, :], hid[g - AHEAD][:], start=False, stop=(done_a == HID_BLOCKS - 1)
                 )
-            if 0 < r < N_PIECES and a in (AHEAD, AHEAD + 2, AHEAD + 4):
-                second_norm_step(r - 1, (a - AHEAD) // 2)
-        for step in range(3):
-            second_norm_step(N_PIECES - 1, step)
+
+        flip(0)
+        z1_bias = centred(bo_over_sc, "z1_bias")
+        z2_bias = centred(b2_sb, "z2_bias")
+        sums(0)
+        divide_1(0)
+        for r, which in second_run:
+            open_by_pos(r, which)
+        residual_pos(0)
+        residual_pos(1)
+        for r, which in second_run:
+            close_by_table(r, which)
+        residual_table(0)
+        residual_table(1)
+        divide_2(0)
+        divide_3(0)
+        flip(1)
+        divide_4(0)
+        project_out(0)
+        sums(1)
+        first_norm_1(0)
+        flip(2)
+        divide_1(1)
+        first_norm_2(0)
+        flip(3)
+        sums(2)
+        first_norm_3(0)
+        divide_2(1)
+        divide_3(1)
+        first_norm_4(0)
+        first_norm_5(0)
+
+        w2_mean = held.tile([P, HID_BLOCKS], F32, name="w2_mean")
+        w2_c = held.tile([P, HID_BLOCKS, P], BF16, name="w2_c")
+        for a in range(0, HID_BLOCKS, 4):
+            nc.vector.tensor_reduce(out=w2_mean[:, a : a + 4], in_=w2_sb[:, a : a + 4, :], axis=mybir.AxisListType.X, op=ALU.add)
+        nc.vector.tensor_scalar(out=w2_mean[:], in0=w2_mean[:], scalar1=1.0 / P, scalar2=None, op0=ALU.mult)
+        for a in range(HID_BLOCKS):
+            nc.vector.tensor_scalar(
+                out=w2_c[:, a, :], in0=w2_sb[:, a, :], scalar1=w2_mean[:, a : a + 1], scalar2=None, op0=ALU.subtract
+            )
+
+        after_sums = (
+            divide_1, divide_2, divide_3, residual, divide_4, pause, project_out,
+            first_norm_1, pause, first_norm_2, first_norm_3, first_norm_4, first_norm_5,
+        )
+        second_norm = (second_norm_1, pause, second_norm_2, second_norm_3, second_norm_4, second_norm_5)
+        waiting = [(step, 1) for step in after_sums[after_sums.index(divide_4) :]]
+        waiting += [(step, 2) for step in after_sums]
+        written = 0
+        for g in range(N_PIECES * HID_BLOCKS + AHEAD):
+            hidden_block(g)
+            done_r, done_a = divmod(g - AHEAD, HID_BLOCKS)
+            if done_r >= 0 and done_a == HID_BLOCKS - 1:
+                waiting += [(step, done_r) for step in second_norm]
+                if done_r == 0:
+                    waiting += [(step, 3) for step in (sums,) + after_sums]
+            if written < len(waiting):
+                step, r = waiting[written]
+                step(r)
+                written += 1
+        for step, r in waiting[written:]:
+            step(r)

@@ -89,22 +89,23 @@ def tile_decoderonlyaft_b_kernel(
             source = two[:, 0 : P * N].rearrange("a (p j) -> p a j", j=N)[:, :, 0:BAND]
             return load(queue, [P, 2, BAND], F32, "wb%d" % m, source)
 
-        pos_sb = load(nc.sync, [P, N], BF16, "pos_sb", pos)
+        table_sb = load(nc.sync, [P, S], BF16, "table_sb", table)
         w_sb[KEY] = load(nc.scalar, [P, P], BF16, "wk_sb", wk)
-        wb[0] = load_band(nc.sync, 0)
-        w_sb[VAL] = load(nc.scalar, [P, P], BF16, "wv_sb", wv)
         offsets = held.tile([P, N // 16], U16, name="offsets")
         nc.sync.dma_start(offsets[:], offs)
+        w_sb[VAL] = load(nc.scalar, [P, P], BF16, "wv_sb", wv)
+        wb[0] = load_band(nc.sync, 0)
         wb[1] = load_band(nc.scalar, 1)
-        table_sb = load(nc.sync, [P, S], BF16, "table_sb", table)
-        bv_sb = load(nc.sync, [P, 1], F32, "bv_sb", bv)
         wb[2] = load_band(nc.sync, 2)
-        bq_sb = load(nc.sync, [P, 1], F32, "bq_sb", bq)
+        pos_sb = load(nc.sync, [P, N], BF16, "pos_sb", pos)
+        bv_sb = load(nc.sync, [P, 1], F32, "bv_sb", bv)
         wb[3] = load_band(nc.sync, 3)
+        bq_sb = load(nc.sync, [P, 1], F32, "bq_sb", bq)
         wb[4] = load_band(nc.sync, 4)
+        wb[5] = load_band(nc.sync, 5)
         bo_sb = load(nc.sync, [P, 1], F32, "bo_sb", bo)
-        for m in range(5, BLOCKS // 2):
-            wb[m] = load_band(nc.sync, m)
+        wb[6] = load_band(nc.sync, 6)
+        wb[7] = load_band(nc.sync, 7)
         wo_sb = load(nc.sync, [P, P], BF16, "wo_sb", wo)
         w1_sb = load(nc.sync, [P, HID], BF16, "w1_sb", w1)
         w2_sb = load(nc.sync, [P, HID_BLOCKS, P], BF16, "w2_sb", w2.rearrange("(p a) c -> p a c", a=HID_BLOCKS))
@@ -131,7 +132,12 @@ def tile_decoderonlyaft_b_kernel(
         nc.vector.memset(eps2[:], EPS)
 
         def project_pos(bank, weights, r, start, stop):
-            nc.tensor.matmul(bank[:], weights, pos_sb[:, piece(r)], start=start, stop=stop)
+            for half in range(2):
+                cols = slice(half * PIECE // 2, (half + 1) * PIECE // 2)
+                nc.tensor.matmul(
+                    bank[:, cols], weights, pos_sb[:, piece(r)][:, cols],
+                    start=(start and half == 0), stop=(stop and half == 1),
+                )
 
         def project_table(bank, weights, r, start, stop):
             looked_up = table_sb[:].indirect(offsets[:, r * OFFS_COLS : (r + 1) * OFFS_COLS])
@@ -167,42 +173,19 @@ def tile_decoderonlyaft_b_kernel(
             nc.scalar.activation(out=ew[u][:], in_=wb[m][:, a, first : first + seen_blocks * P], func=ACT.Exp)
             if seen_blocks == 3:
                 edges = ew[u][:].rearrange("p (b x) -> p b x", x=P)[:, 0:3:2, :]
-                nc.vector.tensor_tensor(out=edges, in0=edges, in1=edge_mask[:], op=ALU.mult)
+                nc.gpsimd.tensor_tensor(out=edges, in0=edges, in1=edge_mask[:], op=ALU.mult)
             else:
-                nc.vector.tensor_tensor(out=ew[u][:, block(0)], in0=ew[u][:, block(0)], in1=edge_mask[:, 0, :], op=ALU.mult)
+                nc.gpsimd.tensor_tensor(out=ew[u][:, block(0)], in0=ew[u][:, block(0)], in1=edge_mask[:, 0, :], op=ALU.mult)
 
-        first_run = ((0, KEY), (0, VAL), (1, KEY), (2, KEY), (3, KEY), (0, QRY), (1, QRY), (2, QRY))
-        second_run = ((1, VAL), (2, VAL), (3, VAL))
-
-        def open_by_pos(r, which):
-            banks[r, which] = new_bank("proj")
-            project_pos(banks[r, which], w_twice[which][:], r, start=True, stop=False)
-
-        def close_by_table(r, which):
-            project_table(banks[r, which], w_sb[which][:], r, start=False, stop=True)
-            finish(r, which)
-
+        first_run = [(r, which) for r in range(N_PIECES) for which in (KEY, VAL)]
         for r, which in first_run:
-            open_by_pos(r, which)
+            banks[r, which] = new_bank("proj")
+            project_table(banks[r, which], w_sb[which][:], r, start=True, stop=False)
         nc.vector.tensor_scalar(out=bv_over_sc[:], in0=bv_sb[:], scalar1=1.0 / SC, scalar2=None, op0=ALU.mult)
         nc.vector.tensor_scalar(out=neg_bq[:], in0=bq_sb[:], scalar1=-1.0, scalar2=None, op0=ALU.mult)
         for r, which in first_run:
-            close_by_table(r, which)
-        banks[3, QRY] = new_bank("proj")
-        project_table(banks[3, QRY], w_sb[QRY][:], 3, start=True, stop=False)
-        project_pos(banks[3, QRY], w_twice[QRY][:], 3, start=False, stop=True)
-        finish(3, QRY)
-        for u in range(BLOCKS):
-            band_weights(u)
-
-        wo_sum = held.tile([P, 1], F32, name="wo_sum")
-        nc.vector.tensor_reduce(out=wo_sum[:], in_=wo_sb[:], axis=mybir.AxisListType.X, op=ALU.add)
-        wo_mean = held.tile([P, 1], F32, name="wo_mean")
-        nc.vector.tensor_scalar(out=wo_mean[:], in0=wo_sum[:], scalar1=1.0 / P, scalar2=None, op0=ALU.mult)
-        wo_c = held.tile([P, P], BF16, name="wo_c")
-        nc.vector.tensor_scalar(out=wo_c[:], in0=wo_sb[:], scalar1=wo_mean[:, 0:1], scalar2=None, op0=ALU.subtract)
-        bo_over_sc = held.tile([P, 1], F32, name="bo_over_sc")
-        nc.vector.tensor_scalar(out=bo_over_sc[:], in0=bo_sb[:], scalar1=1.0 / SC, scalar2=None, op0=ALU.mult)
+            project_pos(banks[r, which], w_twice[which][:], r, start=False, stop=True)
+            finish(r, which)
 
         kT, num, den, divisor, inverse_root, inverse, y, z1, n1 = {}, {}, {}, {}, {}, {}, {}, {}, {}
 
@@ -261,32 +244,48 @@ def tile_decoderonlyaft_b_kernel(
 
         squares, var, rstd, scaled = {}, {}, {}, {}
 
+        def parts(which_norm, r):
+            if which_norm == 2 and r == N_PIECES - 1:
+                return (slice(0, PIECE // 2), slice(PIECE // 2, PIECE))
+            return (slice(0, PIECE),)
+
         def norm_1(which_norm, r, z, bias):
             squares[which_norm, r] = work.tile([P, PIECE], BF16, name="squares")
-            nc.scalar.activation(out=squares[which_norm, r][:], in_=z[:], func=ACT.Square, bias=bias[:, 0:1])
+            for cols in parts(which_norm, r):
+                nc.scalar.activation(
+                    out=squares[which_norm, r][:, cols], in_=z[:, cols], func=ACT.Square, bias=bias[:, 0:1]
+                )
 
         def norm_2(which_norm, r):
-            var[which_norm, r] = new_bank("var")
-            nc.tensor.matmul(var[which_norm, r][:], mean_w[:], squares[which_norm, r][:], start=True, stop=True)
+            for cols in parts(which_norm, r):
+                var[which_norm, r, cols.start] = new_bank("var")
+                nc.tensor.matmul(
+                    var[which_norm, r, cols.start][:, cols], mean_w[:], squares[which_norm, r][:, cols],
+                    start=True, stop=True,
+                )
 
         def norm_3(which_norm, r, eps):
             rstd[which_norm, r] = work.tile([P, PIECE], F32, name="rstd")
-            nc.scalar.activation(
-                out=rstd[which_norm, r][:], in_=var[which_norm, r][:], func=ACT.Abs_reciprocal_sqrt, bias=eps[:, 0:1]
-            )
+            for cols in parts(which_norm, r):
+                nc.scalar.activation(
+                    out=rstd[which_norm, r][:, cols], in_=var[which_norm, r, cols.start][:, cols],
+                    func=ACT.Abs_reciprocal_sqrt, bias=eps[:, 0:1],
+                )
 
         def norm_4(which_norm, r, z, bias):
             scaled[which_norm, r] = work.tile([P, PIECE], F32, name="scaled")
-            nc.vector.scalar_tensor_tensor(
-                out=scaled[which_norm, r][:], in0=z[:], scalar=bias[:, 0:1], in1=rstd[which_norm, r][:],
-                op0=ALU.add, op1=ALU.mult,
-            )
+            for cols in parts(which_norm, r):
+                nc.vector.scalar_tensor_tensor(
+                    out=scaled[which_norm, r][:, cols], in0=z[:, cols], scalar=bias[:, 0:1],
+                    in1=rstd[which_norm, r][:, cols], op0=ALU.add, op1=ALU.mult,
+                )
 
         def norm_5(which_norm, r, normal):
-            nc.vector.tensor_scalar(
-                out=normal[:], in0=scaled[which_norm, r][:], scalar1=gain[:, 0:1], scalar2=shift[:, 0:1],
-                op0=ALU.mult, op1=ALU.add,
-            )
+            for cols in parts(which_norm, r):
+                nc.vector.tensor_scalar(
+                    out=normal[:, cols], in0=scaled[which_norm, r][:, cols], scalar1=gain[:, 0:1],
+                    scalar2=shift[:, 0:1], op0=ALU.mult, op1=ALU.add,
+                )
 
         def first_norm_1(r):
             norm_1(1, r, z1[r], z1_bias)
@@ -321,7 +320,8 @@ def tile_decoderonlyaft_b_kernel(
         def second_norm_5(r):
             result = work.tile([P, PIECE], F32, name="result")
             norm_5(2, r, result)
-            nc.sync.dma_start(out[:, piece(r)], result[:])
+            for cols in parts(2, r):
+                nc.sync.dma_start(out[:, piece(r)][:, cols], result[:, cols])
 
         def pause(r):
             pass
@@ -356,30 +356,44 @@ def tile_decoderonlyaft_b_kernel(
                 )
 
         flip(0)
+        for r in range(N_PIECES):
+            banks[r, QRY] = new_bank("proj")
+            project_pos(banks[r, QRY], w_twice[QRY][:], r, start=True, stop=False)
+        flip(1)
+        for r in range(N_PIECES):
+            project_table(banks[r, QRY], w_sb[QRY][:], r, start=False, stop=True)
+            finish(r, QRY)
+        for u in range(BLOCKS):
+            band_weights(u)
+
+        wo_sum = held.tile([P, 1], F32, name="wo_sum")
+        nc.vector.tensor_reduce(out=wo_sum[:], in_=wo_sb[:], axis=mybir.AxisListType.X, op=ALU.add)
+        wo_mean = held.tile([P, 1], F32, name="wo_mean")
+        nc.vector.tensor_scalar(out=wo_mean[:], in0=wo_sum[:], scalar1=1.0 / P, scalar2=None, op0=ALU.mult)
+        wo_c = held.tile([P, P], BF16, name="wo_c")
+        nc.vector.tensor_scalar(out=wo_c[:], in0=wo_sb[:], scalar1=wo_mean[:, 0:1], scalar2=None, op0=ALU.subtract)
+        bo_over_sc = held.tile([P, 1], F32, name="bo_over_sc")
+        nc.vector.tensor_scalar(out=bo_over_sc[:], in0=bo_sb[:], scalar1=1.0 / SC, scalar2=None, op0=ALU.mult)
+
         z1_bias = centred(bo_over_sc, "z1_bias")
         z2_bias = centred(b2_sb, "z2_bias")
         sums(0)
         divide_1(0)
-        for r, which in second_run:
-            open_by_pos(r, which)
-        residual_pos(0)
-        residual_pos(1)
-        for r, which in second_run:
-            close_by_table(r, which)
-        residual_table(0)
-        residual_table(1)
+        flip(2)
+        flip(3)
+        sums(1)
         divide_2(0)
         divide_3(0)
-        flip(1)
+        residual_pos(0)
+        residual_pos(1)
+        residual_table(0)
+        residual_table(1)
         divide_4(0)
         project_out(0)
-        sums(1)
-        first_norm_1(0)
-        flip(2)
         divide_1(1)
-        first_norm_2(0)
-        flip(3)
+        first_norm_1(0)
         sums(2)
+        first_norm_2(0)
         first_norm_3(0)
         divide_2(1)
         divide_3(1)

@@ -197,10 +197,11 @@ def tile_decoderonlyaft_b_kernel(
             kT[r] = held.tile([P, 2 * PIECE], BF16, name="kT%d" % r)
             nc.vector.tensor_copy(kT[r][:], flipped[:])
 
-        def sums(r):
-            num[r] = new_bank("num")
-            den[r] = new_bank("den")
-            for b in range(BLOCKS_PER_PIECE):
+        def sums(r, token_blocks=range(BLOCKS_PER_PIECE)):
+            if token_blocks[0] == 0:
+                num[r] = new_bank("num")
+                den[r] = new_bank("den")
+            for b in token_blocks:
                 j = r * BLOCKS_PER_PIECE + b
                 attended = [u for u in (j - 2, j - 1, j) if u >= 0]
                 for u in attended:
@@ -210,23 +211,35 @@ def tile_decoderonlyaft_b_kernel(
                     nc.tensor.matmul(num[r][:, block(b)], kT[ur][:, block(2 * ub)], seen, start=first, stop=last)
                     nc.tensor.matmul(den[r][:, block(b)], kT[ur][:, block(2 * ub + 1)], seen, start=first, stop=last)
 
+        def parts(which_norm, r):
+            if (which_norm, r) in ((1, 0), (1, 1), (2, N_PIECES - 1)):
+                return (slice(0, PIECE // 2), slice(PIECE // 2, PIECE))
+            return (slice(0, PIECE),)
+
         def divide_1(r):
             divisor[r] = work.tile([P, PIECE], F32, name="divisor")
-            nc.vector.scalar_tensor_tensor(
-                out=divisor[r][:], in0=eq[r][:], scalar=1.0, in1=den[r][:], op0=ALU.add, op1=ALU.mult
-            )
+            for cols in parts(1, r):
+                nc.vector.scalar_tensor_tensor(
+                    out=divisor[r][:, cols], in0=eq[r][:, cols], scalar=1.0, in1=den[r][:, cols],
+                    op0=ALU.add, op1=ALU.mult,
+                )
 
         def divide_2(r):
             inverse_root[r] = work.tile([P, PIECE], F32, name="inverse_root")
-            nc.scalar.activation(out=inverse_root[r][:], in_=divisor[r][:], func=ACT.Abs_reciprocal_sqrt)
+            for cols in parts(1, r):
+                nc.scalar.activation(
+                    out=inverse_root[r][:, cols], in_=divisor[r][:, cols], func=ACT.Abs_reciprocal_sqrt
+                )
 
         def divide_3(r):
             inverse[r] = work.tile([P, PIECE], F32, name="inverse")
-            nc.scalar.activation(out=inverse[r][:], in_=inverse_root[r][:], func=ACT.Square)
+            for cols in parts(1, r):
+                nc.scalar.activation(out=inverse[r][:, cols], in_=inverse_root[r][:, cols], func=ACT.Square)
 
         def divide_4(r):
             y[r] = work.tile([P, PIECE], BF16, name="y")
-            nc.vector.tensor_tensor(out=y[r][:], in0=num[r][:], in1=inverse[r][:], op=ALU.mult)
+            for cols in parts(1, r):
+                nc.vector.tensor_tensor(out=y[r][:, cols], in0=num[r][:, cols], in1=inverse[r][:, cols], op=ALU.mult)
 
         def residual_pos(r):
             z1[r] = new_bank("z1")
@@ -240,14 +253,10 @@ def tile_decoderonlyaft_b_kernel(
             residual_table(r)
 
         def project_out(r):
-            nc.tensor.matmul(z1[r][:], wo_c[:], y[r][:], start=False, stop=True)
+            for cols in parts(1, r):
+                nc.tensor.matmul(z1[r][:, cols], wo_c[:], y[r][:, cols], start=False, stop=(cols.stop == PIECE))
 
         squares, var, rstd, scaled = {}, {}, {}, {}
-
-        def parts(which_norm, r):
-            if which_norm == 2 and r == N_PIECES - 1:
-                return (slice(0, PIECE // 2), slice(PIECE // 2, PIECE))
-            return (slice(0, PIECE),)
 
         def norm_1(which_norm, r, z, bias):
             squares[which_norm, r] = work.tile([P, PIECE], BF16, name="squares")
@@ -355,14 +364,14 @@ def tile_decoderonlyaft_b_kernel(
                     z2[done_r][:], w2_c[:, done_a, :], hid[g - AHEAD][:], start=False, stop=(done_a == HID_BLOCKS - 1)
                 )
 
-        flip(0)
         for r in range(N_PIECES):
             banks[r, QRY] = new_bank("proj")
             project_pos(banks[r, QRY], w_twice[QRY][:], r, start=True, stop=False)
-        flip(1)
+        flip(0)
         for r in range(N_PIECES):
             project_table(banks[r, QRY], w_sb[QRY][:], r, start=False, stop=True)
             finish(r, QRY)
+        flip(1)
         for u in range(BLOCKS):
             band_weights(u)
 
@@ -392,11 +401,13 @@ def tile_decoderonlyaft_b_kernel(
         project_out(0)
         divide_1(1)
         first_norm_1(0)
-        sums(2)
+        sums(2, range(0, 2))
         first_norm_2(0)
+        sums(2, range(2, 4))
         first_norm_3(0)
         divide_2(1)
         divide_3(1)
+        residual(2)
         first_norm_4(0)
         first_norm_5(0)
 
@@ -416,7 +427,7 @@ def tile_decoderonlyaft_b_kernel(
         )
         second_norm = (second_norm_1, pause, second_norm_2, second_norm_3, second_norm_4, second_norm_5)
         waiting = [(step, 1) for step in after_sums[after_sums.index(divide_4) :]]
-        waiting += [(step, 2) for step in after_sums]
+        waiting += [(step, 2) for step in after_sums if step is not residual]
         written = 0
         for g in range(N_PIECES * HID_BLOCKS + AHEAD):
             hidden_block(g)

@@ -371,7 +371,8 @@ def tile_decoderonlyaft_b_kernel(
         for r in range(N_PIECES):
             project_table(banks[r, QRY], w_sb[QRY][:], r, start=False, stop=True)
             finish(r, QRY)
-        flip(1)
+        for r in range(1, N_PIECES):
+            flip(r)
         for u in range(BLOCKS):
             band_weights(u)
 
@@ -388,15 +389,13 @@ def tile_decoderonlyaft_b_kernel(
         z2_bias = centred(b2_sb, "z2_bias")
         sums(0)
         divide_1(0)
-        flip(2)
-        flip(3)
-        sums(1)
-        divide_2(0)
-        divide_3(0)
         residual_pos(0)
         residual_pos(1)
         residual_table(0)
         residual_table(1)
+        sums(1)
+        divide_2(0)
+        divide_3(0)
         divide_4(0)
         project_out(0)
         divide_1(1)
@@ -410,6 +409,9 @@ def tile_decoderonlyaft_b_kernel(
         residual(2)
         first_norm_4(0)
         first_norm_5(0)
+        sums(3)
+        divide_1(2)
+        divide_1(3)
 
         w2_mean = held.tile([P, HID_BLOCKS], F32, name="w2_mean")
         w2_c = held.tile([P, HID_BLOCKS, P], BF16, name="w2_c")
@@ -427,7 +429,7 @@ def tile_decoderonlyaft_b_kernel(
         )
         second_norm = (second_norm_1, pause, second_norm_2, second_norm_3, second_norm_4, second_norm_5)
         waiting = [(step, 1) for step in after_sums[after_sums.index(divide_4) :]]
-        waiting += [(step, 2) for step in after_sums if step is not residual]
+        waiting += [(step, 2) for step in after_sums if step not in (residual, divide_1)]
         written = 0
         for g in range(N_PIECES * HID_BLOCKS + AHEAD):
             hidden_block(g)
@@ -435,7 +437,7 @@ def tile_decoderonlyaft_b_kernel(
             if done_r >= 0 and done_a == HID_BLOCKS - 1:
                 waiting += [(step, done_r) for step in second_norm]
                 if done_r == 0:
-                    waiting += [(step, 3) for step in (sums,) + after_sums]
+                    waiting += [(step, 3) for step in after_sums if step is not divide_1]
             if written < len(waiting):
                 step, r = waiting[written]
                 step(r)

@@ -197,19 +197,26 @@ def tile_decoderonlyaft_b_kernel(
             kT[r] = held.tile([P, 2 * PIECE], BF16, name="kT%d" % r)
             nc.vector.tensor_copy(kT[r][:], flipped[:])
 
-        def sums(r, token_blocks=range(BLOCKS_PER_PIECE)):
-            if token_blocks[0] == 0:
+        def sum_terms(r):
+            first = r * BLOCKS_PER_PIECE
+            terms = [(first, 0, 2), (first + 1, 1, 2), (first + 1, 3, 3), (first + 2, 2, 3), (first + 3, 3, 3)]
+            if r > 0:
+                terms += [(first - 1, 0, 1), (first - 2, 0, 0)]
+            return terms
+
+        def sums(r, part=slice(None)):
+            terms = sum_terms(r)
+            if terms[part][0] == terms[0]:
                 num[r] = new_bank("num")
                 den[r] = new_bank("den")
-            for b in token_blocks:
-                j = r * BLOCKS_PER_PIECE + b
-                attended = [u for u in (j - 2, j - 1, j) if u >= 0]
-                for u in attended:
-                    ur, ub = divmod(u, BLOCKS_PER_PIECE)
-                    seen = ew[u][:, block(j - u)]
-                    first, last = u == attended[0], u == attended[-1]
-                    nc.tensor.matmul(num[r][:, block(b)], kT[ur][:, block(2 * ub)], seen, start=first, stop=last)
-                    nc.tensor.matmul(den[r][:, block(b)], kT[ur][:, block(2 * ub + 1)], seen, start=first, stop=last)
+            for u, b0, b1 in terms[part]:
+                ur, ub = divmod(u, BLOCKS_PER_PIECE)
+                j0 = r * BLOCKS_PER_PIECE + b0
+                seen = ew[u][:, (j0 - u) * P : (j0 - u + b1 - b0 + 1) * P]
+                cols = slice(b0 * P, (b1 + 1) * P)
+                opens, closes = (u, b0, b1) == terms[0], (u, b0, b1) == terms[-1]
+                nc.tensor.matmul(num[r][:, cols], kT[ur][:, block(2 * ub)], seen, start=opens, stop=closes)
+                nc.tensor.matmul(den[r][:, cols], kT[ur][:, block(2 * ub + 1)], seen, start=opens, stop=closes)
 
         def parts(which_norm, r):
             if (which_norm, r) in ((1, 0), (1, 1), (2, N_PIECES - 1)):
@@ -389,27 +396,27 @@ def tile_decoderonlyaft_b_kernel(
         z2_bias = centred(b2_sb, "z2_bias")
         sums(0)
         divide_1(0)
+        sums(1)
         residual_pos(0)
         residual_pos(1)
         residual_table(0)
         residual_table(1)
-        sums(1)
         divide_2(0)
         divide_3(0)
         divide_4(0)
         project_out(0)
         divide_1(1)
         first_norm_1(0)
-        sums(2, range(0, 2))
+        sums(2, slice(0, 3))
         first_norm_2(0)
-        sums(2, range(2, 4))
+        sums(2, slice(3, None))
         first_norm_3(0)
         divide_2(1)
         divide_3(1)
-        residual(2)
         first_norm_4(0)
         first_norm_5(0)
         sums(3)
+        residual(2)
         divide_1(2)
         divide_1(3)
 

@@ -131,13 +131,16 @@ def tile_decoderonlyaft_b_kernel(
         eps2 = held.tile([P, 1], F32, name="eps2")
         nc.vector.memset(eps2[:], EPS)
 
+        def project_pos_half(bank, weights, r, half, start, stop):
+            cols = slice(half * PIECE // 2, (half + 1) * PIECE // 2)
+            nc.tensor.matmul(
+                bank[:, cols], weights, pos_sb[:, piece(r)][:, cols],
+                start=(start and half == 0), stop=(stop and half == 1),
+            )
+
         def project_pos(bank, weights, r, start, stop):
             for half in range(2):
-                cols = slice(half * PIECE // 2, (half + 1) * PIECE // 2)
-                nc.tensor.matmul(
-                    bank[:, cols], weights, pos_sb[:, piece(r)][:, cols],
-                    start=(start and half == 0), stop=(stop and half == 1),
-                )
+                project_pos_half(bank, weights, r, half, start, stop)
 
         def project_table(bank, weights, r, start, stop):
             looked_up = table_sb[:].indirect(offsets[:, r * OFFS_COLS : (r + 1) * OFFS_COLS])
@@ -189,11 +192,15 @@ def tile_decoderonlyaft_b_kernel(
 
         kT, num, den, divisor, inverse_root, inverse, y, z1, n1 = {}, {}, {}, {}, {}, {}, {}, {}, {}
 
-        def flip(r):
+        def flip_between(r, matmuls):
             flipped = psum.tile([P, 2 * PIECE], BF16, name="flipped", tag="bank")
-            for b in range(BLOCKS_PER_PIECE):
-                nc.tensor.transpose(flipped[:, block(2 * b)], ekv[r][:, block(b)], ident[:])
-                nc.tensor.transpose(flipped[:, block(2 * b + 1)], ek[r][:, block(b)], ident[:])
+            n_transposes = 2 * BLOCKS_PER_PIECE
+            share = (n_transposes + len(matmuls) - 1) // len(matmuls)
+            for m, matmul_step in enumerate(matmuls):
+                matmul_step()
+                for i in range(m * share, min((m + 1) * share, n_transposes)):
+                    source = (ekv[r], ek[r])[i % 2]
+                    nc.tensor.transpose(flipped[:, block(i)], source[:, block(i // 2)], ident[:])
             kT[r] = held.tile([P, 2 * PIECE], BF16, name="kT%d" % r)
             nc.vector.tensor_copy(kT[r][:], flipped[:])
 
@@ -204,19 +211,29 @@ def tile_decoderonlyaft_b_kernel(
                 terms += [(first - 1, 0, 1), (first - 2, 0, 0)]
             return terms
 
-        def sums(r, part=slice(None)):
+        def sum_term(r, term, bank, which):
+            u, b0, b1 = term
             terms = sum_terms(r)
-            if terms[part][0] == terms[0]:
-                num[r] = new_bank("num")
-                den[r] = new_bank("den")
-            for u, b0, b1 in terms[part]:
-                ur, ub = divmod(u, BLOCKS_PER_PIECE)
-                j0 = r * BLOCKS_PER_PIECE + b0
-                seen = ew[u][:, (j0 - u) * P : (j0 - u + b1 - b0 + 1) * P]
-                cols = slice(b0 * P, (b1 + 1) * P)
-                opens, closes = (u, b0, b1) == terms[0], (u, b0, b1) == terms[-1]
-                nc.tensor.matmul(num[r][:, cols], kT[ur][:, block(2 * ub)], seen, start=opens, stop=closes)
-                nc.tensor.matmul(den[r][:, cols], kT[ur][:, block(2 * ub + 1)], seen, start=opens, stop=closes)
+            ur, ub = divmod(u, BLOCKS_PER_PIECE)
+            j0 = r * BLOCKS_PER_PIECE + b0
+            seen = ew[u][:, (j0 - u) * P : (j0 - u + b1 - b0 + 1) * P]
+            nc.tensor.matmul(
+                bank[:, b0 * P : (b1 + 1) * P], kT[ur][:, block(2 * ub + which)], seen,
+                start=(term == terms[0]), stop=(term == terms[-1]),
+            )
+
+        def sum_steps(r):
+            num[r] = new_bank("num")
+            den[r] = new_bank("den")
+            steps = []
+            for term in sum_terms(r):
+                steps.append(lambda term=term: sum_term(r, term, num[r], 0))
+                steps.append(lambda term=term: sum_term(r, term, den[r], 1))
+            return steps
+
+        def run(steps):
+            for step in steps:
+                step()
 
         def parts(which_norm, r):
             if (which_norm, r) in ((1, 0), (1, 1), (2, N_PIECES - 1)):
@@ -371,15 +388,18 @@ def tile_decoderonlyaft_b_kernel(
                     z2[done_r][:], w2_c[:, done_a, :], hid[g - AHEAD][:], start=False, stop=(done_a == HID_BLOCKS - 1)
                 )
 
-        for r in range(N_PIECES):
-            banks[r, QRY] = new_bank("proj")
-            project_pos(banks[r, QRY], w_twice[QRY][:], r, start=True, stop=False)
-        flip(0)
-        for r in range(N_PIECES):
+        def open_query(r, half):
+            project_pos_half(banks[r, QRY], w_twice[QRY][:], r, half, start=True, stop=False)
+
+        def close_query(r):
             project_table(banks[r, QRY], w_sb[QRY][:], r, start=False, stop=True)
             finish(r, QRY)
-        for r in range(1, N_PIECES):
-            flip(r)
+
+        for r in range(N_PIECES):
+            banks[r, QRY] = new_bank("proj")
+            open_query(r, 0)
+        flip_between(0, [lambda r=r: open_query(r, 1) for r in range(N_PIECES)])
+        flip_between(1, [lambda r=r: close_query(r) for r in range(N_PIECES)])
         for u in range(BLOCKS):
             band_weights(u)
 
@@ -394,9 +414,9 @@ def tile_decoderonlyaft_b_kernel(
 
         z1_bias = centred(bo_over_sc, "z1_bias")
         z2_bias = centred(b2_sb, "z2_bias")
-        sums(0)
+        flip_between(2, sum_steps(0))
         divide_1(0)
-        sums(1)
+        flip_between(3, sum_steps(1))
         residual_pos(0)
         residual_pos(1)
         residual_table(0)
@@ -407,15 +427,16 @@ def tile_decoderonlyaft_b_kernel(
         project_out(0)
         divide_1(1)
         first_norm_1(0)
-        sums(2, slice(0, 3))
+        sums_of_2 = sum_steps(2)
+        run(sums_of_2[:6])
         first_norm_2(0)
-        sums(2, slice(3, None))
+        run(sums_of_2[6:])
         first_norm_3(0)
         divide_2(1)
         divide_3(1)
         first_norm_4(0)
         first_norm_5(0)
-        sums(3)
+        run(sum_steps(3))
         residual(2)
         divide_1(2)
         divide_1(3)

@@ -25,6 +25,7 @@ BAND = WIN + P
 HID_BLOCKS = HID // P
 KEY, VAL, QRY = 0, 1, 2
 AHEAD = 4
+EARLY_BAND = 4
 
 FLOPS = 2 * P * P * N * 4 + 2 * 2 * P * WIN * N + 2 * 2 * P * HID * N
 BYTES = (
@@ -100,12 +101,12 @@ def tile_decoderonlyaft_b_kernel(
         pos_sb = load(nc.sync, [P, N], BF16, "pos_sb", pos)
         bv_sb = load(nc.sync, [P, 1], F32, "bv_sb", bv)
         wb[3] = load_band(nc.sync, 3)
-        bq_sb = load(nc.sync, [P, 1], F32, "bq_sb", bq)
         wb[4] = load_band(nc.sync, 4)
         wb[5] = load_band(nc.sync, 5)
         bo_sb = load(nc.sync, [P, 1], F32, "bo_sb", bo)
         wb[6] = load_band(nc.sync, 6)
         wb[7] = load_band(nc.sync, 7)
+        bq_sb = load(nc.sync, [P, 1], F32, "bq_sb", bq)
         wo_sb = load(nc.sync, [P, P], BF16, "wo_sb", wo)
         w1_sb = load(nc.sync, [P, HID], BF16, "w1_sb", w1)
         w2_sb = load(nc.sync, [P, HID_BLOCKS, P], BF16, "w2_sb", w2.rearrange("(p a) c -> p a c", a=HID_BLOCKS))
@@ -185,7 +186,9 @@ def tile_decoderonlyaft_b_kernel(
             banks[r, which] = new_bank("proj")
             project_table(banks[r, which], w_sb[which][:], r, start=True, stop=False)
         nc.vector.tensor_scalar(out=bv_over_sc[:], in0=bv_sb[:], scalar1=1.0 / SC, scalar2=None, op0=ALU.mult)
-        nc.vector.tensor_scalar(out=neg_bq[:], in0=bq_sb[:], scalar1=-1.0, scalar2=None, op0=ALU.mult)
+        nc.scalar.mul(neg_bq[:], bq_sb[:], -1.0)
+        for u in range(EARLY_BAND):
+            band_weights(u)
         for r, which in first_run:
             project_pos(banks[r, which], w_twice[which][:], r, start=False, stop=True)
             finish(r, which)
@@ -400,7 +403,7 @@ def tile_decoderonlyaft_b_kernel(
             open_query(r, 0)
         flip_between(0, [lambda r=r: open_query(r, 1) for r in range(N_PIECES)])
         flip_between(1, [lambda r=r: close_query(r) for r in range(N_PIECES)])
-        for u in range(BLOCKS):
+        for u in range(EARLY_BAND, BLOCKS):
             band_weights(u)
 
         wo_sum = held.tile([P, 1], F32, name="wo_sum")

@@ -239,9 +239,8 @@ def tile_decoderonlyaft_b_kernel(
                 step()
 
         def parts(which_norm, r):
-            if (which_norm, r) in ((1, 0), (1, 1), (2, N_PIECES - 1)):
-                return (slice(0, PIECE // 2), slice(PIECE // 2, PIECE))
-            return (slice(0, PIECE),)
+            n_parts = {(1, 0): 4, (1, 1): 2, (2, N_PIECES - 1): 2}.get((which_norm, r), 1)
+            return [slice(i * PIECE // n_parts, (i + 1) * PIECE // n_parts) for i in range(n_parts)]
 
         def divide_1(r):
             divisor[r] = work.tile([P, PIECE], F32, name="divisor")

@@ -426,13 +426,13 @@ def tile_decoderonlyaft_b_kernel(
         divide_2(0)
         divide_3(0)
         divide_4(0)
+        sums_of_2 = sum_steps(2)
+        run(sums_of_2[:6])
         project_out(0)
         divide_1(1)
         first_norm_1(0)
-        sums_of_2 = sum_steps(2)
-        run(sums_of_2[:6])
-        first_norm_2(0)
         run(sums_of_2[6:])
+        first_norm_2(0)
         first_norm_3(0)
         divide_2(1)
         divide_3(1)

@@ -269,7 +269,7 @@ def tile_decoderonlyaft_b_kernel(
 
         def residual_pos(r):
             z1[r] = new_bank("z1")
-            project_pos(z1[r], center2[:], r, start=True, stop=False)
+            nc.tensor.matmul(z1[r][:], center2[:], pos_sb[:, piece(r)], start=True, stop=False)
 
         def residual_table(r):
             project_table(z1[r], center[:], r, start=False, stop=False)

@@ -26,6 +26,8 @@ HID_BLOCKS = HID // P
 KEY, VAL, QRY = 0, 1, 2
 AHEAD = 4
 EARLY_BAND = 4
+SQUARE = 32
+GROUPS = PIECE // SQUARE
 
 FLOPS = 2 * P * P * N * 4 + 2 * 2 * P * WIN * N + 2 * 2 * P * HID * N
 BYTES = (
@@ -127,6 +129,16 @@ def tile_decoderonlyaft_b_kernel(
         nc.vector.tensor_scalar(out=center2[:], in0=center_f[:], scalar1=2.0, scalar2=None, op0=ALU.mult)
         mean_w = held.tile([P, P], BF16, name="mean_w")
         nc.vector.memset(mean_w[:], 1.0 / P)
+        same_place = held.tile([P, SQUARE], F32, name="same_place")
+        nc.vector.tensor_reduce(
+            out=same_place[:], in_=ident_f[:].rearrange("p (q k) -> p k q", k=SQUARE), axis=mybir.AxisListType.X, op=ALU.add
+        )
+        fold_w = held.tile([P, P], BF16, name="fold_w")
+        nc.vector.tensor_scalar(
+            out=fold_w[:].rearrange("p (q k) -> p q k", k=SQUARE),
+            in0=same_place[:].unsqueeze(1).to_broadcast([P, P // SQUARE, SQUARE]),
+            scalar1=1.0 / P, scalar2=None, op0=ALU.mult,
+        )
         eps1 = held.tile([P, 1], F32, name="eps1")
         nc.vector.memset(eps1[:], EPS / (SC * SC))
         eps2 = held.tile([P, 1], F32, name="eps2")
@@ -285,7 +297,7 @@ def tile_decoderonlyaft_b_kernel(
         squares, var, rstd, scaled = {}, {}, {}, {}
 
         def norm_1(which_norm, r, z, bias):
-            squares[which_norm, r] = work.tile([P, PIECE], BF16, name="squares")
+            squares[which_norm, r] = work.tile([P, PIECE], BF16, name="squares", align_bytes=64)
             for cols in parts(which_norm, r):
                 nc.scalar.activation(
                     out=squares[which_norm, r][:, cols], in_=z[:, cols], func=ACT.Square, bias=bias[:, 0:1]
@@ -300,7 +312,7 @@ def tile_decoderonlyaft_b_kernel(
                 )
 
         def norm_3(which_norm, r, eps):
-            rstd[which_norm, r] = work.tile([P, PIECE], F32, name="rstd")
+            rstd[which_norm, r] = work.tile([P, PIECE], F32, name="rstd", align_bytes=64)
             for cols in parts(which_norm, r):
                 nc.scalar.activation(
                     out=rstd[which_norm, r][:, cols], in_=var[which_norm, r, cols.start][:, cols],
@@ -349,6 +361,38 @@ def tile_decoderonlyaft_b_kernel(
         def second_norm_3(r):
             norm_3(2, r, eps2)
 
+        squares_turned, partial, var_folded, rstd_folded = {}, {}, {}, {}
+
+        def in_groups(ap):
+            return ap.rearrange("p (t k) -> p t k", k=SQUARE)
+
+        def second_norm_2_turn(r):
+            squares_turned[r] = work.tile([P, PIECE], BF16, name="squares_turned", align_bytes=64)
+            nc.vector.transpose(squares_turned[r][:], squares[2, r][:])
+
+        def second_norm_2_vector(r):
+            partial[r] = work.tile([P, GROUPS], BF16, name="partial")
+            with nc.allow_low_precision(reason="a sum of 32 squares, rounded once before the matmul that it enters"):
+                nc.vector.tensor_reduce(
+                    out=partial[r][:], in_=in_groups(squares_turned[r][:]), axis=mybir.AxisListType.X, op=ALU.add
+                )
+
+        def second_norm_2_tensor(r):
+            var_folded[r] = new_bank("var_folded")
+            nc.tensor.matmul(var_folded[r][:, 0:GROUPS], fold_w[:], partial[r][:], start=True, stop=True)
+
+        def second_norm_3_scalar(r):
+            rstd_folded[r] = work.tile([P, PIECE], F32, name="rstd_folded", align_bytes=64)
+            nc.scalar.activation(
+                out=in_groups(rstd_folded[r][:]),
+                in_=var_folded[r][:, 0:GROUPS].unsqueeze(2).to_broadcast([P, GROUPS, SQUARE]),
+                func=ACT.Abs_reciprocal_sqrt, bias=eps2[:, 0:1],
+            )
+
+        def second_norm_3_vector(r):
+            rstd[2, r] = work.tile([P, PIECE], F32, name="rstd", align_bytes=64)
+            nc.vector.transpose(rstd[2, r][:], rstd_folded[r][:])
+
         def second_norm_4(r):
             norm_4(2, r, z2[r], z2_bias)
 
@@ -377,7 +421,7 @@ def tile_decoderonlyaft_b_kernel(
                 hid_ps = new_bank("hid_ps")
                 nc.tensor.matmul(hid_ps[:], w1_sb[:, a : HID : HID_BLOCKS], n1[r][:], start=True, stop=True)
                 hid[g] = hidden.tile([P, PIECE], BF16, name="hid")
-                if a % 3 == 0:
+                if a % 2 == 0:
                     nc.scalar.activation(out=hid[g][:], in_=hid_ps[:], func=ACT.Relu, bias=b1_sb[:, a : a + 1])
                 else:
                     nc.vector.tensor_scalar(
@@ -458,6 +502,10 @@ def tile_decoderonlyaft_b_kernel(
             first_norm_1, pause, first_norm_2, first_norm_3, first_norm_4, first_norm_5,
         )
         second_norm = (second_norm_1, pause, second_norm_2, second_norm_3, second_norm_4, second_norm_5)
+        second_norm_beside = (
+            second_norm_1, second_norm_2_turn, second_norm_2_vector, pause, pause, pause, second_norm_2_tensor, second_norm_3_scalar, second_norm_3_vector,
+            second_norm_4, second_norm_5,
+        )
         waiting = [(step, 1) for step in after_sums[after_sums.index(divide_4) :]]
         waiting += [(step, 2) for step in after_sums if step not in (residual, divide_1)]
         written = 0
@@ -465,7 +513,7 @@ def tile_decoderonlyaft_b_kernel(
             hidden_block(g)
             done_r, done_a = divmod(g - AHEAD, HID_BLOCKS)
             if done_r >= 0 and done_a == HID_BLOCKS - 1:
-                waiting += [(step, done_r) for step in second_norm]
+                waiting += [(step, done_r) for step in (second_norm if done_r == N_PIECES - 1 else second_norm_beside)]
                 if done_r == 0:
                     waiting += [(step, 3) for step in after_sums if step is not divide_1]
             if written < len(waiting):

@@ -319,6 +319,41 @@ def tile_decoderonlyaft_b_kernel(
                     func=ACT.Abs_reciprocal_sqrt, bias=eps[:, 0:1],
                 )
 
+        squares_turned, partial, var_folded, rstd_folded = {}, {}, {}, {}
+
+        def in_groups(ap):
+            return ap.rearrange("p (t k) -> p t k", k=SQUARE)
+
+        def fold_1(which_norm, r):
+            squares_turned[which_norm, r] = work.tile([P, PIECE], BF16, name="squares_turned", align_bytes=64)
+            nc.vector.transpose(squares_turned[which_norm, r][:], squares[which_norm, r][:])
+
+        def fold_2(which_norm, r):
+            partial[which_norm, r] = work.tile([P, GROUPS], BF16, name="partial")
+            with nc.allow_low_precision(reason="a sum of 32 squares, rounded once before the matmul that it enters"):
+                nc.vector.tensor_reduce(
+                    out=partial[which_norm, r][:], in_=in_groups(squares_turned[which_norm, r][:]),
+                    axis=mybir.AxisListType.X, op=ALU.add,
+                )
+
+        def fold_3(which_norm, r):
+            var_folded[which_norm, r] = new_bank("var_folded")
+            nc.tensor.matmul(
+                var_folded[which_norm, r][:, 0:GROUPS], fold_w[:], partial[which_norm, r][:], start=True, stop=True
+            )
+
+        def fold_4(which_norm, r, eps):
+            rstd_folded[which_norm, r] = work.tile([P, PIECE], F32, name="rstd_folded", align_bytes=64)
+            nc.scalar.activation(
+                out=in_groups(rstd_folded[which_norm, r][:]),
+                in_=var_folded[which_norm, r][:, 0:GROUPS].unsqueeze(2).to_broadcast([P, GROUPS, SQUARE]),
+                func=ACT.Abs_reciprocal_sqrt, bias=eps[:, 0:1],
+            )
+
+        def fold_5(which_norm, r):
+            rstd[which_norm, r] = work.tile([P, PIECE], F32, name="rstd", align_bytes=64)
+            nc.vector.transpose(rstd[which_norm, r][:], rstd_folded[which_norm, r][:])
+
         def norm_4(which_norm, r, z, bias):
             scaled[which_norm, r] = work.tile([P, PIECE], F32, name="scaled")
             for cols in parts(which_norm, r):
@@ -360,38 +395,6 @@ def tile_decoderonlyaft_b_kernel(
 
         def second_norm_3(r):
             norm_3(2, r, eps2)
-
-        squares_turned, partial, var_folded, rstd_folded = {}, {}, {}, {}
-
-        def in_groups(ap):
-            return ap.rearrange("p (t k) -> p t k", k=SQUARE)
-
-        def second_norm_2_turn(r):
-            squares_turned[r] = work.tile([P, PIECE], BF16, name="squares_turned", align_bytes=64)
-            nc.vector.transpose(squares_turned[r][:], squares[2, r][:])
-
-        def second_norm_2_vector(r):
-            partial[r] = work.tile([P, GROUPS], BF16, name="partial")
-            with nc.allow_low_precision(reason="a sum of 32 squares, rounded once before the matmul that it enters"):
-                nc.vector.tensor_reduce(
-                    out=partial[r][:], in_=in_groups(squares_turned[r][:]), axis=mybir.AxisListType.X, op=ALU.add
-                )
-
-        def second_norm_2_tensor(r):
-            var_folded[r] = new_bank("var_folded")
-            nc.tensor.matmul(var_folded[r][:, 0:GROUPS], fold_w[:], partial[r][:], start=True, stop=True)
-
-        def second_norm_3_scalar(r):
-            rstd_folded[r] = work.tile([P, PIECE], F32, name="rstd_folded", align_bytes=64)
-            nc.scalar.activation(
-                out=in_groups(rstd_folded[r][:]),
-                in_=var_folded[r][:, 0:GROUPS].unsqueeze(2).to_broadcast([P, GROUPS, SQUARE]),
-                func=ACT.Abs_reciprocal_sqrt, bias=eps2[:, 0:1],
-            )
-
-        def second_norm_3_vector(r):
-            rstd[2, r] = work.tile([P, PIECE], F32, name="rstd", align_bytes=64)
-            nc.vector.transpose(rstd[2, r][:], rstd_folded[r][:])
 
         def second_norm_4(r):
             norm_4(2, r, z2[r], z2_bias)
@@ -497,28 +500,35 @@ def tile_decoderonlyaft_b_kernel(
                 out=w2_c[:, a, :], in0=w2_sb[:, a, :], scalar1=w2_mean[:, a : a + 1], scalar2=None, op0=ALU.subtract
             )
 
-        after_sums = (
-            divide_1, divide_2, divide_3, residual, divide_4, pause, project_out,
-            first_norm_1, pause, first_norm_2, first_norm_3, first_norm_4, first_norm_5,
-        )
-        second_norm = (second_norm_1, pause, second_norm_2, second_norm_3, second_norm_4, second_norm_5)
-        second_norm_beside = (
-            second_norm_1, second_norm_2_turn, second_norm_2_vector, pause, pause, pause, second_norm_2_tensor, second_norm_3_scalar, second_norm_3_vector,
-            second_norm_4, second_norm_5,
-        )
-        waiting = [(step, 1) for step in after_sums[after_sums.index(divide_4) :]]
-        waiting += [(step, 2) for step in after_sums if step not in (residual, divide_1)]
-        written = 0
+        def fold_steps(which_norm, eps):
+            return (
+                lambda r: fold_1(which_norm, r), lambda r: fold_2(which_norm, r), pause, pause, pause,
+                lambda r: fold_3(which_norm, r), lambda r: fold_4(which_norm, r, eps), lambda r: fold_5(which_norm, r),
+            )
+
+        division = (divide_2, divide_3, divide_4)
+        to_first_norm = (residual, project_out, first_norm_1)
+        first_norm_soon = (pause, first_norm_2, first_norm_3, first_norm_4, first_norm_5)
+        first_norm_beside = fold_steps(1, eps1) + (first_norm_4, first_norm_5)
+        second_norm_soon = (second_norm_1, pause, second_norm_2, second_norm_3, second_norm_4, second_norm_5)
+        second_norm_beside = (second_norm_1,) + fold_steps(2, eps2) + (second_norm_4, second_norm_5)
+        divisions = [(divide_4, 1)] + [(step, r) for r in (2, 3) for step in division]
+        mixing = [(step, 1) for step in (pause, pause, project_out, first_norm_1) + first_norm_soon]
+        mixing += [(step, 2) for step in to_first_norm + first_norm_beside if step is not residual]
+        mixing += [(step, 3) for step in to_first_norm + first_norm_beside]
+        norms = []
+        rows = (divisions, mixing, norms)
+        written = [0, 0, 0]
         for g in range(N_PIECES * HID_BLOCKS + AHEAD):
             hidden_block(g)
             done_r, done_a = divmod(g - AHEAD, HID_BLOCKS)
             if done_r >= 0 and done_a == HID_BLOCKS - 1:
-                waiting += [(step, done_r) for step in (second_norm if done_r == N_PIECES - 1 else second_norm_beside)]
-                if done_r == 0:
-                    waiting += [(step, 3) for step in after_sums if step is not divide_1]
-            if written < len(waiting):
-                step, r = waiting[written]
+                norms += [(step, done_r) for step in (second_norm_soon if done_r == N_PIECES - 1 else second_norm_beside)]
+            for i, row in enumerate(rows):
+                if written[i] < len(row):
+                    step, r = row[written[i]]
+                    step(r)
+                    written[i] += 1
+        for i, row in enumerate(rows):
+            for step, r in row[written[i] :]:
                 step(r)
-                written += 1
-        for step, r in waiting[written:]:
-            step(r)

@@ -24,7 +24,7 @@ BLOCKS_PER_PIECE = PIECE // P
 BAND = WIN + P
 HID_BLOCKS = HID // P
 KEY, VAL, QRY = 0, 1, 2
-AHEAD = 4
+AHEAD = 6
 EARLY_BAND = 4
 SQUARE = 32
 GROUPS = PIECE // SQUARE
@@ -46,7 +46,7 @@ def tile_decoderonlyaft_b_kernel(
     with ExitStack() as ctx:
         held = ctx.enter_context(tc.tile_pool(name="held", bufs=1))
         work = ctx.enter_context(tc.tile_pool(name="work", bufs=4))
-        hidden = ctx.enter_context(tc.tile_pool(name="hidden", bufs=6))
+        hidden = ctx.enter_context(tc.tile_pool(name="hidden", bufs=AHEAD + 2))
         psum = ctx.enter_context(tc.psum_pool(name="psum", bufs=8))
 
         def new_bank(name):

@@ -424,7 +424,7 @@ def tile_decoderonlyaft_b_kernel(
                 hid_ps = new_bank("hid_ps")
                 nc.tensor.matmul(hid_ps[:], w1_sb[:, a : HID : HID_BLOCKS], n1[r][:], start=True, stop=True)
                 hid[g] = hidden.tile([P, PIECE], BF16, name="hid")
-                if a % 2 == 0:
+                if a % 2 == 0 or a == HID_BLOCKS - 1:
                     nc.scalar.activation(out=hid[g][:], in_=hid_ps[:], func=ACT.Relu, bias=b1_sb[:, a : a + 1])
                 else:
                     nc.vector.tensor_scalar(

@@ -28,6 +28,9 @@ AHEAD = 6
 EARLY_BAND = 4
 SQUARE = 32
 GROUPS = PIECE // SQUARE
+LAST = N_PIECES - 1
+REST = 128
+MAIN = PIECE - REST
 
 FLOPS = 2 * P * P * N * 4 + 2 * 2 * P * WIN * N + 2 * 2 * P * HID * N
 BYTES = (
@@ -251,7 +254,9 @@ def tile_decoderonlyaft_b_kernel(
                 step()
 
         def parts(which_norm, r):
-            n_parts = {(1, 0): 4, (1, 1): 2, (2, N_PIECES - 1): 2}.get((which_norm, r), 1)
+            if (which_norm, r) == (2, LAST):
+                return [slice(0, MAIN // 2), slice(MAIN // 2, MAIN), slice(MAIN, PIECE)]
+            n_parts = {(1, 0): 4, (1, 1): 2}.get((which_norm, r), 1)
             return [slice(i * PIECE // n_parts, (i + 1) * PIECE // n_parts) for i in range(n_parts)]
 
         def divide_1(r):
@@ -296,24 +301,26 @@ def tile_decoderonlyaft_b_kernel(
 
         squares, var, rstd, scaled = {}, {}, {}, {}
 
-        def norm_1(which_norm, r, z, bias):
-            squares[which_norm, r] = work.tile([P, PIECE], BF16, name="squares", align_bytes=64)
-            for cols in parts(which_norm, r):
+        def norm_1(which_norm, r, z, bias, only=None):
+            if (which_norm, r) not in squares:
+                squares[which_norm, r] = work.tile([P, PIECE], BF16, name="squares", align_bytes=64)
+            for cols in only or parts(which_norm, r):
                 nc.scalar.activation(
                     out=squares[which_norm, r][:, cols], in_=z[:, cols], func=ACT.Square, bias=bias[:, 0:1]
                 )
 
-        def norm_2(which_norm, r):
-            for cols in parts(which_norm, r):
+        def norm_2(which_norm, r, only=None):
+            for cols in only or parts(which_norm, r):
                 var[which_norm, r, cols.start] = new_bank("var")
                 nc.tensor.matmul(
                     var[which_norm, r, cols.start][:, cols], mean_w[:], squares[which_norm, r][:, cols],
                     start=True, stop=True,
                 )
 
-        def norm_3(which_norm, r, eps):
-            rstd[which_norm, r] = work.tile([P, PIECE], F32, name="rstd", align_bytes=64)
-            for cols in parts(which_norm, r):
+        def norm_3(which_norm, r, eps, only=None):
+            if (which_norm, r) not in rstd:
+                rstd[which_norm, r] = work.tile([P, PIECE], F32, name="rstd", align_bytes=64)
+            for cols in only or parts(which_norm, r):
                 nc.scalar.activation(
                     out=rstd[which_norm, r][:, cols], in_=var[which_norm, r, cols.start][:, cols],
                     func=ACT.Abs_reciprocal_sqrt, bias=eps[:, 0:1],
@@ -354,16 +361,17 @@ def tile_decoderonlyaft_b_kernel(
             rstd[which_norm, r] = work.tile([P, PIECE], F32, name="rstd", align_bytes=64)
             nc.vector.transpose(rstd[which_norm, r][:], rstd_folded[which_norm, r][:])
 
-        def norm_4(which_norm, r, z, bias):
-            scaled[which_norm, r] = work.tile([P, PIECE], F32, name="scaled")
-            for cols in parts(which_norm, r):
+        def norm_4(which_norm, r, z, bias, only=None):
+            if (which_norm, r) not in scaled:
+                scaled[which_norm, r] = work.tile([P, PIECE], F32, name="scaled")
+            for cols in only or parts(which_norm, r):
                 nc.vector.scalar_tensor_tensor(
                     out=scaled[which_norm, r][:, cols], in0=z[:, cols], scalar=bias[:, 0:1],
                     in1=rstd[which_norm, r][:, cols], op0=ALU.add, op1=ALU.mult,
                 )
 
-        def norm_5(which_norm, r, normal):
-            for cols in parts(which_norm, r):
+        def norm_5(which_norm, r, normal, only=None):
+            for cols in only or parts(which_norm, r):
                 nc.vector.tensor_scalar(
                     out=normal[:, cols], in0=scaled[which_norm, r][:, cols], scalar1=gain[:, 0:1],
                     scalar2=shift[:, 0:1], op0=ALU.mult, op1=ALU.add,
@@ -385,25 +393,32 @@ def tile_decoderonlyaft_b_kernel(
             n1[r] = held.tile([P, PIECE], BF16, name="n1_%d" % r)
             norm_5(1, r, n1[r])
 
-        z2, hid = {}, {}
+        z2, hid, result = {}, {}, {}
 
-        def second_norm_1(r):
-            norm_1(2, r, z2[r], z2_bias)
+        def z2_bank(r, cols):
+            return z2["rest"] if r == LAST and cols.start >= MAIN else z2[r]
 
-        def second_norm_2(r):
-            norm_2(2, r)
+        def second_norm_1(r, only=None):
+            for cols in only or parts(2, r):
+                norm_1(2, r, z2_bank(r, cols), z2_bias, [cols])
 
-        def second_norm_3(r):
-            norm_3(2, r, eps2)
+        def second_norm_2(r, only=None):
+            norm_2(2, r, only)
 
-        def second_norm_4(r):
-            norm_4(2, r, z2[r], z2_bias)
+        def second_norm_3(r, only=None):
+            norm_3(2, r, eps2, only)
 
-        def second_norm_5(r):
-            result = work.tile([P, PIECE], F32, name="result")
-            norm_5(2, r, result)
-            for cols in parts(2, r):
-                nc.sync.dma_start(out[:, piece(r)][:, cols], result[:, cols])
+        def second_norm_4(r, only=None):
+            for cols in only or parts(2, r):
+                norm_4(2, r, z2_bank(r, cols), z2_bias, [cols])
+
+        def second_norm_5(r, only=None):
+            if r not in result:
+                result[r] = work.tile([P, PIECE], F32, name="result")
+            norm_5(2, r, result[r], only)
+            for cols in only or parts(2, r):
+                queue = nc.scalar if r == LAST and cols.start >= MAIN else nc.sync
+                queue.dma_start(out[:, piece(r)][:, cols], result[r][:, cols])
 
         def pause(r):
             pass
@@ -415,15 +430,22 @@ def tile_decoderonlyaft_b_kernel(
             nc.vector.tensor_copy(t[:], vec_ps[:, 0:1])
             return t
 
+        def in_stream(r):
+            return slice(0, MAIN if r == LAST else PIECE)
+
         def hidden_block(g):
             r, a = divmod(g, HID_BLOCKS)
             if r < N_PIECES:
                 if a == 0:
                     z2[r] = new_bank("z2")
-                    nc.tensor.matmul(z2[r][:], center[:], n1[r][:], start=True, stop=False)
+                    cols = in_stream(r)
+                    nc.tensor.matmul(z2[r][:, cols], center[:], n1[r][:, cols], start=True, stop=False)
                 hid_ps = new_bank("hid_ps")
                 nc.tensor.matmul(hid_ps[:], w1_sb[:, a : HID : HID_BLOCKS], n1[r][:], start=True, stop=True)
-                hid[g] = hidden.tile([P, PIECE], BF16, name="hid")
+                if r == LAST:
+                    hid[g] = held.tile([P, PIECE], BF16, name="hid_last%d" % a)
+                else:
+                    hid[g] = hidden.tile([P, PIECE], BF16, name="hid")
                 if a % 2 == 0 or a == HID_BLOCKS - 1:
                     nc.scalar.activation(out=hid[g][:], in_=hid_ps[:], func=ACT.Relu, bias=b1_sb[:, a : a + 1])
                 else:
@@ -433,9 +455,24 @@ def tile_decoderonlyaft_b_kernel(
                     )
             if g >= AHEAD:
                 done_r, done_a = divmod(g - AHEAD, HID_BLOCKS)
+                cols = in_stream(done_r)
                 nc.tensor.matmul(
-                    z2[done_r][:], w2_c[:, done_a, :], hid[g - AHEAD][:], start=False, stop=(done_a == HID_BLOCKS - 1)
+                    z2[done_r][:, cols], w2_c[:, done_a, :], hid[g - AHEAD][:, cols],
+                    start=False, stop=(done_a == HID_BLOCKS - 1),
                 )
+
+        def rest_steps():
+            z2["rest"] = new_bank("z2_rest")
+            cols = slice(MAIN, PIECE)
+            steps = [lambda: nc.tensor.matmul(z2["rest"][:, cols], center[:], n1[LAST][:, cols], start=True, stop=False)]
+            for a in range(HID_BLOCKS):
+                steps.append(
+                    lambda a=a: nc.tensor.matmul(
+                        z2["rest"][:, cols], w2_c[:, a, :], hid[LAST * HID_BLOCKS + a][:, cols],
+                        start=False, stop=(a == HID_BLOCKS - 1),
+                    )
+                )
+            return steps
 
         def open_query(r, half):
             project_pos_half(banks[r, QRY], w_twice[QRY][:], r, half, start=True, stop=False)
@@ -510,7 +547,6 @@ def tile_decoderonlyaft_b_kernel(
         to_first_norm = (residual, project_out, first_norm_1)
         first_norm_soon = (pause, first_norm_2, first_norm_3, first_norm_4, first_norm_5)
         first_norm_beside = fold_steps(1, eps1) + (first_norm_4, first_norm_5)
-        second_norm_soon = (second_norm_1, pause, second_norm_2, second_norm_3, second_norm_4, second_norm_5)
         second_norm_beside = (second_norm_1,) + fold_steps(2, eps2) + (second_norm_4, second_norm_5)
         divisions = [(divide_4, 1)] + [(step, r) for r in (2, 3) for step in division]
         mixing = [(step, 1) for step in (pause, pause, project_out, first_norm_1) + first_norm_soon]
@@ -522,8 +558,8 @@ def tile_decoderonlyaft_b_kernel(
         for g in range(N_PIECES * HID_BLOCKS + AHEAD):
             hidden_block(g)
             done_r, done_a = divmod(g - AHEAD, HID_BLOCKS)
-            if done_r >= 0 and done_a == HID_BLOCKS - 1:
-                norms += [(step, done_r) for step in (second_norm_soon if done_r == N_PIECES - 1 else second_norm_beside)]
+            if 0 <= done_r < LAST and done_a == HID_BLOCKS - 1:
+                norms += [(step, done_r) for step in second_norm_beside]
             for i, row in enumerate(rows):
                 if written[i] < len(row):
                     step, r = row[written[i]]
@@ -532,3 +568,19 @@ def tile_decoderonlyaft_b_kernel(
         for i, row in enumerate(rows):
             for step, r in row[written[i] :]:
                 step(r)
+
+        first_half, second_half, rest = parts(2, LAST)
+        rest_matmuls = rest_steps()
+        third = len(rest_matmuls) // 3
+        second_norm_1(LAST, [first_half, second_half])
+        run(rest_matmuls[:third])
+        second_norm_2(LAST, [first_half])
+        run(rest_matmuls[third : 2 * third])
+        second_norm_2(LAST, [second_half])
+        run(rest_matmuls[2 * third :])
+        for step in (second_norm_3, second_norm_4, second_norm_5):
+            step(LAST, [first_half])
+        for step in (second_norm_3, second_norm_4, second_norm_5):
+            step(LAST, [second_half])
+        for step in (second_norm_1, second_norm_2, second_norm_3, second_norm_4, second_norm_5):
+            step(LAST, [rest])

@@ -196,7 +196,8 @@ def tile_decoderonlyaft_b_kernel(
             else:
                 nc.gpsimd.tensor_tensor(out=ew[u][:, block(0)], in0=ew[u][:, block(0)], in1=edge_mask[:, 0, :], op=ALU.mult)
 
-        first_run = [(r, which) for r in range(N_PIECES) for which in (KEY, VAL)]
+        first_run = [(r, which) for r in range(LAST) for which in (KEY, VAL)]
+        second_run = [(LAST, KEY), (LAST, VAL)] + [(r, QRY) for r in range(N_PIECES)]
         for r, which in first_run:
             banks[r, which] = new_bank("proj")
             project_table(banks[r, which], w_sb[which][:], r, start=True, stop=False)
@@ -474,18 +475,18 @@ def tile_decoderonlyaft_b_kernel(
                 )
             return steps
 
-        def open_query(r, half):
-            project_pos_half(banks[r, QRY], w_twice[QRY][:], r, half, start=True, stop=False)
+        def open_bank(r, which, half):
+            project_pos_half(banks[r, which], w_twice[which][:], r, half, start=True, stop=False)
 
-        def close_query(r):
-            project_table(banks[r, QRY], w_sb[QRY][:], r, start=False, stop=True)
-            finish(r, QRY)
+        def close_bank(r, which):
+            project_table(banks[r, which], w_sb[which][:], r, start=False, stop=True)
+            finish(r, which)
 
-        for r in range(N_PIECES):
-            banks[r, QRY] = new_bank("proj")
-            open_query(r, 0)
-        flip_between(0, [lambda r=r: open_query(r, 1) for r in range(N_PIECES)])
-        flip_between(1, [lambda r=r: close_query(r) for r in range(N_PIECES)])
+        for r, which in second_run:
+            banks[r, which] = new_bank("proj")
+            open_bank(r, which, 0)
+        flip_between(0, [lambda r=r, which=which: open_bank(r, which, 1) for r, which in second_run])
+        flip_between(1, [lambda r=r, which=which: close_bank(r, which) for r, which in second_run])
         for u in range(EARLY_BAND, BLOCKS):
             band_weights(u)
 

@@ -115,6 +115,8 @@ def tile_decoderonlyaft_b_kernel(
         wo_sb = load(nc.sync, [P, P], BF16, "wo_sb", wo)
         w1_sb = load(nc.sync, [P, HID], BF16, "w1_sb", w1)
         w2_sb = load(nc.sync, [P, HID_BLOCKS, P], BF16, "w2_sb", w2.rearrange("(p a) c -> p a c", a=HID_BLOCKS))
+        bo_row = load(nc.sync, [P, P], F32, "bo_row", bo.rearrange("c o -> (c o)").partition_broadcast(P))
+        b2_row = load(nc.sync, [P, P], F32, "b2_row", b2.rearrange("c o -> (c o)").partition_broadcast(P))
         b2_sb = load(nc.gpsimd, [P, 1], F32, "b2_sb", b2)
         gain = load(nc.gpsimd, [P, 1], F32, "gain", ln_gain)
         shift = load(nc.gpsimd, [P, 1], F32, "shift", ln_shift)
@@ -424,11 +426,15 @@ def tile_decoderonlyaft_b_kernel(
         def pause(r):
             pass
 
-        def centred(vec, name):
-            vec_ps = new_bank("vec_ps")
-            nc.tensor.matmul(vec_ps[:, 0:1], center_f[:], vec[:], start=True, stop=True)
+        def centred(vec, row, factor, name):
+            total = held.tile([P, 1], F32, name=name + "_total")
+            nc.vector.tensor_reduce(out=total[:], in_=row[:], axis=mybir.AxisListType.X, op=ALU.add)
+            mean = held.tile([P, 1], F32, name=name + "_mean")
+            nc.vector.tensor_scalar(out=mean[:], in0=total[:], scalar1=1.0 / P, scalar2=None, op0=ALU.mult)
             t = held.tile([P, 1], F32, name=name)
-            nc.vector.tensor_copy(t[:], vec_ps[:, 0:1])
+            nc.vector.tensor_scalar(
+                out=t[:], in0=vec[:], scalar1=mean[:, 0:1], scalar2=factor, op0=ALU.subtract, op1=ALU.mult
+            )
             return t
 
         def in_stream(r):
@@ -496,14 +502,12 @@ def tile_decoderonlyaft_b_kernel(
         nc.vector.tensor_scalar(out=wo_mean[:], in0=wo_sum[:], scalar1=1.0 / P, scalar2=None, op0=ALU.mult)
         wo_c = held.tile([P, P], BF16, name="wo_c")
         nc.vector.tensor_scalar(out=wo_c[:], in0=wo_sb[:], scalar1=wo_mean[:, 0:1], scalar2=None, op0=ALU.subtract)
-        bo_over_sc = held.tile([P, 1], F32, name="bo_over_sc")
-        nc.vector.tensor_scalar(out=bo_over_sc[:], in0=bo_sb[:], scalar1=1.0 / SC, scalar2=None, op0=ALU.mult)
 
-        z1_bias = centred(bo_over_sc, "z1_bias")
-        z2_bias = centred(b2_sb, "z2_bias")
         flip_between(2, sum_steps(0))
         divide_1(0)
         flip_between(3, sum_steps(1))
+        z1_bias = centred(bo_sb, bo_row, 1.0 / SC, "z1_bias")
+        z2_bias = centred(b2_sb, b2_row, 1.0, "z2_bias")
         residual_pos(0)
         residual_pos(1)
         residual_table(0)

@@ -67,8 +67,9 @@ def tile_decoderonlyaft_b_kernel(
             return t
 
         w_sb, wb = {}, {}
-        w_sb[QRY] = load(nc.gpsimd, [P, P], BF16, "wq_sb", wq)
 
+        ident = held.tile([P, P], BF16, name="ident")
+        make_identity(nc, ident[:])
         edge_mask = held.tile([P, 2, P], BF16, name="edge_mask")
         nc.gpsimd.memset(edge_mask[:], 1.0)
         nc.gpsimd.affine_select(
@@ -79,8 +80,6 @@ def tile_decoderonlyaft_b_kernel(
             out=edge_mask[:, 1, :], in_=edge_mask[:, 1, :], compare_op=ALU.is_gt, fill=0.0,
             base=0, pattern=[[-1, P]], channel_multiplier=1,
         )
-        ident = held.tile([P, P], BF16, name="ident")
-        make_identity(nc, ident[:])
         ident_f = held.tile([P, P], F32, name="ident_f")
         make_identity(nc, ident_f[:])
 
@@ -100,6 +99,7 @@ def tile_decoderonlyaft_b_kernel(
         offsets = held.tile([P, N // 16], U16, name="offsets")
         nc.sync.dma_start(offsets[:], offs)
         w_sb[VAL] = load(nc.scalar, [P, P], BF16, "wv_sb", wv)
+        w_sb[QRY] = load(nc.scalar, [P, P], BF16, "wq_sb", wq)
         wb[0] = load_band(nc.sync, 0)
         wb[1] = load_band(nc.scalar, 1)
         wb[2] = load_band(nc.sync, 2)

@@ -443,10 +443,6 @@ def tile_decoderonlyaft_b_kernel(
         def hidden_block(g):
             r, a = divmod(g, HID_BLOCKS)
             if r < N_PIECES:
-                if a == 0:
-                    z2[r] = new_bank("z2")
-                    cols = in_stream(r)
-                    nc.tensor.matmul(z2[r][:, cols], center[:], n1[r][:, cols], start=True, stop=False)
                 hid_ps = new_bank("hid_ps")
                 nc.tensor.matmul(hid_ps[:], w1_sb[:, a : HID : HID_BLOCKS], n1[r][:], start=True, stop=True)
                 if r == LAST:
@@ -463,6 +459,9 @@ def tile_decoderonlyaft_b_kernel(
             if g >= AHEAD:
                 done_r, done_a = divmod(g - AHEAD, HID_BLOCKS)
                 cols = in_stream(done_r)
+                if done_a == 0:
+                    z2[done_r] = new_bank("z2")
+                    nc.tensor.matmul(z2[done_r][:, cols], center[:], n1[done_r][:, cols], start=True, stop=False)
                 nc.tensor.matmul(
                     z2[done_r][:, cols], w2_c[:, done_a, :], hid[g - AHEAD][:, cols],
                     start=False, stop=(done_a == HID_BLOCKS - 1),

@@ -553,7 +553,7 @@ def tile_decoderonlyaft_b_kernel(
         first_norm_beside = fold_steps(1, eps1) + (first_norm_4, first_norm_5)
         second_norm_beside = (second_norm_1,) + fold_steps(2, eps2) + (second_norm_4, second_norm_5)
         divisions = [(divide_4, 1)] + [(step, r) for r in (2, 3) for step in division]
-        mixing = [(step, 1) for step in (pause, pause, project_out, first_norm_1) + first_norm_soon]
+        mixing = [(step, 1) for step in (pause, pause, pause, project_out, first_norm_1) + first_norm_soon]
         mixing += [(step, 2) for step in to_first_norm + first_norm_beside if step is not residual]
         mixing += [(step, 3) for step in to_first_norm + first_norm_beside]
         norms = []

@@ -527,7 +527,6 @@ def tile_decoderonlyaft_b_kernel(
         first_norm_4(0)
         first_norm_5(0)
         run(sum_steps(3))
-        residual(2)
         divide_1(2)
         divide_1(3)
 
@@ -553,7 +552,8 @@ def tile_decoderonlyaft_b_kernel(
         first_norm_beside = fold_steps(1, eps1) + (first_norm_4, first_norm_5)
         second_norm_beside = (second_norm_1,) + fold_steps(2, eps2) + (second_norm_4, second_norm_5)
         divisions = [(divide_4, 1)] + [(step, r) for r in (2, 3) for step in division]
-        mixing = [(step, 1) for step in (pause, pause, pause, project_out, first_norm_1) + first_norm_soon]
+        mixing = [(residual_pos, 2), (residual_table, 2)]
+        mixing += [(step, 1) for step in (pause, project_out, first_norm_1) + first_norm_soon]
         mixing += [(step, 2) for step in to_first_norm + first_norm_beside if step is not residual]
         mixing += [(step, 3) for step in to_first_norm + first_norm_beside]
         norms = []

@@ -548,12 +548,12 @@ def tile_decoderonlyaft_b_kernel(
 
         division = (divide_2, divide_3, divide_4)
         to_first_norm = (residual, project_out, first_norm_1)
-        first_norm_soon = (pause, first_norm_2, first_norm_3, first_norm_4, first_norm_5)
+        first_norm_soon = (pause, pause, first_norm_2, first_norm_3, first_norm_4, first_norm_5)
         first_norm_beside = fold_steps(1, eps1) + (first_norm_4, first_norm_5)
         second_norm_beside = (second_norm_1,) + fold_steps(2, eps2) + (second_norm_4, second_norm_5)
         divisions = [(divide_4, 1)] + [(step, r) for r in (2, 3) for step in division]
         mixing = [(residual_pos, 2), (residual_table, 2)]
-        mixing += [(step, 1) for step in (pause, project_out, first_norm_1) + first_norm_soon]
+        mixing += [(step, 1) for step in (pause, pause, pause, project_out, first_norm_1) + first_norm_soon]
         mixing += [(step, 2) for step in to_first_norm + first_norm_beside if step is not residual]
         mixing += [(step, 3) for step in to_first_norm + first_norm_beside]
         norms = []

@@ -515,17 +515,18 @@ def tile_decoderonlyaft_b_kernel(
         divide_3(0)
         divide_4(0)
         sums_of_2 = sum_steps(2)
-        run(sums_of_2[:6])
+        run(sums_of_2[:4])
         project_out(0)
         divide_1(1)
         first_norm_1(0)
-        run(sums_of_2[6:])
+        run(sums_of_2[4:10])
         first_norm_2(0)
         first_norm_3(0)
         divide_2(1)
         divide_3(1)
         first_norm_4(0)
         first_norm_5(0)
+        run(sums_of_2[10:])
         run(sum_steps(3))
         divide_1(2)
         divide_1(3)

@@ -509,8 +509,10 @@ def tile_decoderonlyaft_b_kernel(
         z2_bias = centred(b2_sb, b2_row, 1.0, "z2_bias")
         residual_pos(0)
         residual_pos(1)
+        residual_pos(2)
         residual_table(0)
         residual_table(1)
+        residual_table(2)
         divide_2(0)
         divide_3(0)
         divide_4(0)
@@ -553,7 +555,7 @@ def tile_decoderonlyaft_b_kernel(
         first_norm_beside = fold_steps(1, eps1) + (first_norm_4, first_norm_5)
         second_norm_beside = (second_norm_1,) + fold_steps(2, eps2) + (second_norm_4, second_norm_5)
         divisions = [(divide_4, 1)] + [(step, r) for r in (2, 3) for step in division]
-        mixing = [(residual_pos, 2), (residual_table, 2)]
+        mixing = [(pause, 2), (pause, 2)]
         mixing += [(step, 1) for step in (pause, pause, pause, project_out, first_norm_1) + first_norm_soon]
         mixing += [(step, 2) for step in to_first_norm + first_norm_beside if step is not residual]
         mixing += [(step, 3) for step in to_first_norm + first_norm_beside]

@@ -420,8 +420,7 @@ def tile_decoderonlyaft_b_kernel(
                 result[r] = work.tile([P, PIECE], F32, name="result")
             norm_5(2, r, result[r], only)
             for cols in only or parts(2, r):
-                queue = nc.scalar if r == LAST and cols.start >= MAIN else nc.sync
-                queue.dma_start(out[:, piece(r)][:, cols], result[r][:, cols])
+                nc.sync.dma_start(out[:, piece(r)][:, cols], result[r][:, cols])
 
         def pause(r):
             pass

import math
from contextlib import ExitStack

import concourse.mybir as mybir
from concourse.masks import make_identity

BF16, F32, U16 = mybir.dt.bfloat16, mybir.dt.float32, mybir.dt.uint16
ALU = mybir.AluOpType
ACT = mybir.ActivationFunctionType

P = 128
S = 1024
N = 2048
HID = 2048
WIN = 256
EPS = 1e-5
SC = 1.0 / math.sqrt(P)

PIECE = 512
N_PIECES = N // PIECE
OFFS_COLS = PIECE // 16
BLOCKS = N // P
BLOCKS_PER_PIECE = PIECE // P
BAND = WIN + P
HID_BLOCKS = HID // P
KEY, VAL, QRY = 0, 1, 2
AHEAD = 6
EARLY_BAND = 4
SQUARE = 32
GROUPS = PIECE // SQUARE
LAST = N_PIECES - 1
REST = 128
MAIN = PIECE - REST

FLOPS = 2 * P * P * N * 4 + 2 * 2 * P * WIN * N + 2 * 2 * P * HID * N
BYTES = (
    2 * (P * S + P * N + 4 * P * P + 2 * P * HID)
    + 4 * (6 * P + HID)
    + 4 * (N * WIN - WIN * (WIN - 1) // 2)
    + 2 * P * (N // 16)
    + 4 * P * N
)


def tile_decoderonlyaft_b_kernel(
    tc, table, pos, wq, bq, wk, wv, bv, wo, bo, wbias, ln_gain, ln_shift, w1, b1, w2, b2, offs, out
):
    nc = tc.nc
    with ExitStack() as ctx:
        held = ctx.enter_context(tc.tile_pool(name="held", bufs=1))
        work = ctx.enter_context(tc.tile_pool(name="work", bufs=4))
        hidden = ctx.enter_context(tc.tile_pool(name="hidden", bufs=AHEAD + 2))
        psum = ctx.enter_context(tc.psum_pool(name="psum", bufs=8))

        def new_bank(name):
            return psum.tile([P, PIECE], F32, name=name, tag="bank")

        def piece(r):
            return slice(r * PIECE, (r + 1) * PIECE)

        def block(b):
            return slice(b * P, (b + 1) * P)

        def load(queue, shape, dtype, name, source):
            t = held.tile(shape, dtype, name=name)
            queue.dma_start(t[:], source)
            return t

        w_sb, wb = {}, {}

        ident = held.tile([P, P], BF16, name="ident")
        make_identity(nc, ident[:])
        edge_mask = held.tile([P, 2, P], BF16, name="edge_mask")
        nc.gpsimd.memset(edge_mask[:], 1.0)
        nc.gpsimd.affine_select(
            out=edge_mask[:, 0, :], in_=edge_mask[:, 0, :], compare_op=ALU.is_ge, fill=0.0,
            base=0, pattern=[[1, P]], channel_multiplier=-1,
        )
        nc.gpsimd.affine_select(
            out=edge_mask[:, 1, :], in_=edge_mask[:, 1, :], compare_op=ALU.is_gt, fill=0.0,
            base=0, pattern=[[-1, P]], channel_multiplier=1,
        )
        ident_f = held.tile([P, P], F32, name="ident_f")
        make_identity(nc, ident_f[:])

        wbias_flat = wbias.rearrange("u j -> (u j)")
        window_step = P * (N + 1)

        def load_band(queue, m):
            if m == BLOCKS // 2 - 1:
                source = wbias[N - 2 * P : N, N - 2 * P : N].rearrange("(a p) x -> p a x", p=P)
                return load(queue, [P, 2, 2 * P], F32, "wb%d" % m, source)
            two = wbias_flat[2 * m * window_step : (2 * m + 2) * window_step].rearrange("(a r) -> a r", r=window_step)
            source = two[:, 0 : P * N].rearrange("a (p j) -> p a j", j=N)[:, :, 0:BAND]
            return load(queue, [P, 2, BAND], F32, "wb%d" % m, source)

        table_sb = load(nc.sync, [P, S], BF16, "table_sb", table)
        w_sb[KEY] = load(nc.scalar, [P, P], BF16, "wk_sb", wk)
        offsets = held.tile([P, N // 16], U16, name="offsets")
        nc.sync.dma_start(offsets[:], offs)
        w_sb[VAL] = load(nc.scalar, [P, P], BF16, "wv_sb", wv)
        w_sb[QRY] = load(nc.scalar, [P, P], BF16, "wq_sb", wq)
        wb[0] = load_band(nc.sync, 0)
        wb[1] = load_band(nc.scalar, 1)
        wb[2] = load_band(nc.sync, 2)
        pos_sb = load(nc.sync, [P, N], BF16, "pos_sb", pos)
        bv_sb = load(nc.sync, [P, 1], F32, "bv_sb", bv)
        wb[3] = load_band(nc.sync, 3)
        wb[4] = load_band(nc.sync, 4)
        wb[5] = load_band(nc.sync, 5)
        bo_sb = load(nc.sync, [P, 1], F32, "bo_sb", bo)
        wb[6] = load_band(nc.sync, 6)
        wb[7] = load_band(nc.sync, 7)
        bq_sb = load(nc.sync, [P, 1], F32, "bq_sb", bq)
        wo_sb = load(nc.sync, [P, P], BF16, "wo_sb", wo)
        w1_sb = load(nc.sync, [P, HID], BF16, "w1_sb", w1)
        w2_sb = load(nc.sync, [P, HID_BLOCKS, P], BF16, "w2_sb", w2.rearrange("(p a) c -> p a c", a=HID_BLOCKS))
        bo_row = load(nc.sync, [P, P], F32, "bo_row", bo.rearrange("c o -> (c o)").partition_broadcast(P))
        b2_row = load(nc.sync, [P, P], F32, "b2_row", b2.rearrange("c o -> (c o)").partition_broadcast(P))
        b2_sb = load(nc.gpsimd, [P, 1], F32, "b2_sb", b2)
        gain = load(nc.gpsimd, [P, 1], F32, "gain", ln_gain)
        shift = load(nc.gpsimd, [P, 1], F32, "shift", ln_shift)
        b1_sb = load(nc.gpsimd, [P, HID_BLOCKS], F32, "b1_sb", b1.rearrange("(p a) o -> p (a o)", a=HID_BLOCKS))

        w_twice = {}
        for which in (KEY, VAL, QRY):
            w_twice[which] = held.tile([P, P], BF16, name="w_twice%d" % which)
            nc.vector.tensor_scalar(out=w_twice[which][:], in0=w_sb[which][:], scalar1=2.0, scalar2=None, op0=ALU.mult)
        center_f = held.tile([P, P], F32, name="center_f")
        nc.vector.tensor_scalar(out=center_f[:], in0=ident_f[:], scalar1=-1.0 / P, scalar2=None, op0=ALU.add)
        center = held.tile([P, P], BF16, name="center")
        nc.vector.tensor_copy(center[:], center_f[:])
        center2 = held.tile([P, P], BF16, name="center2")
        nc.vector.tensor_scalar(out=center2[:], in0=center_f[:], scalar1=2.0, scalar2=None, op0=ALU.mult)
        mean_w = held.tile([P, P], BF16, name="mean_w")
        nc.vector.memset(mean_w[:], 1.0 / P)
        same_place = held.tile([P, SQUARE], F32, name="same_place")
        nc.vector.tensor_reduce(
            out=same_place[:], in_=ident_f[:].rearrange("p (q k) -> p k q", k=SQUARE), axis=mybir.AxisListType.X, op=ALU.add
        )
        fold_w = held.tile([P, P], BF16, name="fold_w")
        nc.vector.tensor_scalar(
            out=fold_w[:].rearrange("p (q k) -> p q k", k=SQUARE),
            in0=same_place[:].unsqueeze(1).to_broadcast([P, P // SQUARE, SQUARE]),
            scalar1=1.0 / P, scalar2=None, op0=ALU.mult,
        )
        eps1 = held.tile([P, 1], F32, name="eps1")
        nc.vector.memset(eps1[:], EPS / (SC * SC))
        eps2 = held.tile([P, 1], F32, name="eps2")
        nc.vector.memset(eps2[:], EPS)

        def project_pos_half(bank, weights, r, half, start, stop):
            cols = slice(half * PIECE // 2, (half + 1) * PIECE // 2)
            nc.tensor.matmul(
                bank[:, cols], weights, pos_sb[:, piece(r)][:, cols],
                start=(start and half == 0), stop=(stop and half == 1),
            )

        def project_pos(bank, weights, r, start, stop):
            for half in range(2):
                project_pos_half(bank, weights, r, half, start, stop)

        def project_table(bank, weights, r, start, stop):
            looked_up = table_sb[:].indirect(offsets[:, r * OFFS_COLS : (r + 1) * OFFS_COLS])
            nc.tensor.matmul(bank[:], weights, looked_up, start=start, stop=stop)

        bv_over_sc = held.tile([P, 1], F32, name="bv_over_sc")
        neg_bq = held.tile([P, 1], F32, name="neg_bq")
        banks, ek, ekv, eq = {}, {}, {}, {}

        def finish(r, which):
            if which == KEY:
                ek[r] = work.tile([P, PIECE], BF16, name="ek")
                nc.scalar.activation(out=ek[r][:], in_=banks[r, which][:], func=ACT.Exp, scale=SC)
            elif which == VAL:
                ekv[r] = work.tile([P, PIECE], BF16, name="ekv")
                nc.vector.scalar_tensor_tensor(
                    out=ekv[r][:], in0=banks[r, which][:], scalar=bv_over_sc[:, 0:1], in1=ek[r][:],
                    op0=ALU.add, op1=ALU.mult,
                )
            else:
                eq[r] = held.tile([P, PIECE], F32, name="eq%d" % r)
                nc.scalar.activation(
                    out=eq[r][:], in_=banks[r, which][:], func=ACT.Exp, scale=-SC, bias=neg_bq[:, 0:1]
                )

        ew = {}

        def band_weights(u):
            m, a = divmod(u, 2)
            seen_blocks = min(BAND, N - P * u) // P
            first = a * P if m == BLOCKS // 2 - 1 else 0
            ew[u] = held.tile([P, seen_blocks * P], BF16, name="ew%d" % u)
            nc.scalar.activation(out=ew[u][:], in_=wb[m][:, a, first : first + seen_blocks * P], func=ACT.Exp)
            if seen_blocks == 3:
                edges = ew[u][:].rearrange("p (b x) -> p b x", x=P)[:, 0:3:2, :]
                nc.gpsimd.tensor_tensor(out=edges, in0=edges, in1=edge_mask[:], op=ALU.mult)
            else:
                nc.gpsimd.tensor_tensor(out=ew[u][:, block(0)], in0=ew[u][:, block(0)], in1=edge_mask[:, 0, :], op=ALU.mult)

        first_run = [(r, which) for r in range(LAST) for which in (KEY, VAL)]
        second_run = [(LAST, KEY), (LAST, VAL)] + [(r, QRY) for r in range(N_PIECES)]
        for r, which in first_run:
            banks[r, which] = new_bank("proj")
            project_table(banks[r, which], w_sb[which][:], r, start=True, stop=False)
        nc.vector.tensor_scalar(out=bv_over_sc[:], in0=bv_sb[:], scalar1=1.0 / SC, scalar2=None, op0=ALU.mult)
        nc.scalar.mul(neg_bq[:], bq_sb[:], -1.0)
        for u in range(EARLY_BAND):
            band_weights(u)
        for r, which in first_run:
            project_pos(banks[r, which], w_twice[which][:], r, start=False, stop=True)
            finish(r, which)

        kT, num, den, divisor, inverse_root, inverse, y, z1, n1 = {}, {}, {}, {}, {}, {}, {}, {}, {}

        def flip_between(r, matmuls):
            flipped = psum.tile([P, 2 * PIECE], BF16, name="flipped", tag="bank")
            n_transposes = 2 * BLOCKS_PER_PIECE
            share = (n_transposes + len(matmuls) - 1) // len(matmuls)
            for m, matmul_step in enumerate(matmuls):
                matmul_step()
                for i in range(m * share, min((m + 1) * share, n_transposes)):
                    source = (ekv[r], ek[r])[i % 2]
                    nc.tensor.transpose(flipped[:, block(i)], source[:, block(i // 2)], ident[:])
            kT[r] = held.tile([P, 2 * PIECE], BF16, name="kT%d" % r)
            nc.vector.tensor_copy(kT[r][:], flipped[:])

        def sum_terms(r):
            first = r * BLOCKS_PER_PIECE
            terms = [(first, 0, 2), (first + 1, 1, 2), (first + 1, 3, 3), (first + 2, 2, 3), (first + 3, 3, 3)]
            if r > 0:
                terms += [(first - 1, 0, 1), (first - 2, 0, 0)]
            return terms

        def sum_term(r, term, bank, which):
            u, b0, b1 = term
            terms = sum_terms(r)
            ur, ub = divmod(u, BLOCKS_PER_PIECE)
            j0 = r * BLOCKS_PER_PIECE + b0
            seen = ew[u][:, (j0 - u) * P : (j0 - u + b1 - b0 + 1) * P]
            nc.tensor.matmul(
                bank[:, b0 * P : (b1 + 1) * P], kT[ur][:, block(2 * ub + which)], seen,
                start=(term == terms[0]), stop=(term == terms[-1]),
            )

        def sum_steps(r):
            num[r] = new_bank("num")
            den[r] = new_bank("den")
            steps = []
            for term in sum_terms(r):
                steps.append(lambda term=term: sum_term(r, term, num[r], 0))
                steps.append(lambda term=term: sum_term(r, term, den[r], 1))
            return steps

        def run(steps):
            for step in steps:
                step()

        def parts(which_norm, r):
            if (which_norm, r) == (2, LAST):
                return [slice(0, MAIN // 2), slice(MAIN // 2, MAIN), slice(MAIN, PIECE)]
            n_parts = {(1, 0): 4, (1, 1): 2}.get((which_norm, r), 1)
            return [slice(i * PIECE // n_parts, (i + 1) * PIECE // n_parts) for i in range(n_parts)]

        def divide_1(r):
            divisor[r] = work.tile([P, PIECE], F32, name="divisor")
            for cols in parts(1, r):
                nc.vector.scalar_tensor_tensor(
                    out=divisor[r][:, cols], in0=eq[r][:, cols], scalar=1.0, in1=den[r][:, cols],
                    op0=ALU.add, op1=ALU.mult,
                )

        def divide_2(r):
            inverse_root[r] = work.tile([P, PIECE], F32, name="inverse_root")
            for cols in parts(1, r):
                nc.scalar.activation(
                    out=inverse_root[r][:, cols], in_=divisor[r][:, cols], func=ACT.Abs_reciprocal_sqrt
                )

        def divide_3(r):
            inverse[r] = work.tile([P, PIECE], F32, name="inverse")
            for cols in parts(1, r):
                nc.scalar.activation(out=inverse[r][:, cols], in_=inverse_root[r][:, cols], func=ACT.Square)

        def divide_4(r):
            y[r] = work.tile([P, PIECE], BF16, name="y")
            for cols in parts(1, r):
                nc.vector.tensor_tensor(out=y[r][:, cols], in0=num[r][:, cols], in1=inverse[r][:, cols], op=ALU.mult)

        def residual_pos(r):
            z1[r] = new_bank("z1")
            nc.tensor.matmul(z1[r][:], center2[:], pos_sb[:, piece(r)], start=True, stop=False)

        def residual_table(r):
            project_table(z1[r], center[:], r, start=False, stop=False)

        def residual(r):
            residual_pos(r)
            residual_table(r)

        def project_out(r):
            for cols in parts(1, r):
                nc.tensor.matmul(z1[r][:, cols], wo_c[:], y[r][:, cols], start=False, stop=(cols.stop == PIECE))

        squares, var, rstd, scaled = {}, {}, {}, {}

        def norm_1(which_norm, r, z, bias, only=None):
            if (which_norm, r) not in squares:
                squares[which_norm, r] = work.tile([P, PIECE], BF16, name="squares", align_bytes=64)
            for cols in only or parts(which_norm, r):
                nc.scalar.activation(
                    out=squares[which_norm, r][:, cols], in_=z[:, cols], func=ACT.Square, bias=bias[:, 0:1]
                )

        def norm_2(which_norm, r, only=None):
            for cols in only or parts(which_norm, r):
                var[which_norm, r, cols.start] = new_bank("var")
                nc.tensor.matmul(
                    var[which_norm, r, cols.start][:, cols], mean_w[:], squares[which_norm, r][:, cols],
                    start=True, stop=True,
                )

        def norm_3(which_norm, r, eps, only=None):
            if (which_norm, r) not in rstd:
                rstd[which_norm, r] = work.tile([P, PIECE], F32, name="rstd", align_bytes=64)
            for cols in only or parts(which_norm, r):
                nc.scalar.activation(
                    out=rstd[which_norm, r][:, cols], in_=var[which_norm, r, cols.start][:, cols],
                    func=ACT.Abs_reciprocal_sqrt, bias=eps[:, 0:1],
                )

        squares_turned, partial, var_folded, rstd_folded = {}, {}, {}, {}

        def in_groups(ap):
            return ap.rearrange("p (t k) -> p t k", k=SQUARE)

        def fold_1(which_norm, r):
            squares_turned[which_norm, r] = work.tile([P, PIECE], BF16, name="squares_turned", align_bytes=64)
            nc.vector.transpose(squares_turned[which_norm, r][:], squares[which_norm, r][:])

        def fold_2(which_norm, r):
            partial[which_norm, r] = work.tile([P, GROUPS], BF16, name="partial")
            with nc.allow_low_precision(reason="a sum of 32 squares, rounded once before the matmul that it enters"):
                nc.vector.tensor_reduce(
                    out=partial[which_norm, r][:], in_=in_groups(squares_turned[which_norm, r][:]),
                    axis=mybir.AxisListType.X, op=ALU.add,
                )

        def fold_3(which_norm, r):
            var_folded[which_norm, r] = new_bank("var_folded")
            nc.tensor.matmul(
                var_folded[which_norm, r][:, 0:GROUPS], fold_w[:], partial[which_norm, r][:], start=True, stop=True
            )

        def fold_4(which_norm, r, eps):
            rstd_folded[which_norm, r] = work.tile([P, PIECE], F32, name="rstd_folded", align_bytes=64)
            nc.scalar.activation(
                out=in_groups(rstd_folded[which_norm, r][:]),
                in_=var_folded[which_norm, r][:, 0:GROUPS].unsqueeze(2).to_broadcast([P, GROUPS, SQUARE]),
                func=ACT.Abs_reciprocal_sqrt, bias=eps[:, 0:1],
            )

        def fold_5(which_norm, r):
            rstd[which_norm, r] = work.tile([P, PIECE], F32, name="rstd", align_bytes=64)
            nc.vector.transpose(rstd[which_norm, r][:], rstd_folded[which_norm, r][:])

        def norm_4(which_norm, r, z, bias, only=None):
            if (which_norm, r) not in scaled:
                scaled[which_norm, r] = work.tile([P, PIECE], F32, name="scaled")
            for cols in only or parts(which_norm, r):
                nc.vector.scalar_tensor_tensor(
                    out=scaled[which_norm, r][:, cols], in0=z[:, cols], scalar=bias[:, 0:1],
                    in1=rstd[which_norm, r][:, cols], op0=ALU.add, op1=ALU.mult,
                )

        def norm_5(which_norm, r, normal, only=None):
            for cols in only or parts(which_norm, r):
                nc.vector.tensor_scalar(
                    out=normal[:, cols], in0=scaled[which_norm, r][:, cols], scalar1=gain[:, 0:1],
                    scalar2=shift[:, 0:1], op0=ALU.mult, op1=ALU.add,
                )

        def first_norm_1(r):
            norm_1(1, r, z1[r], z1_bias)

        def first_norm_2(r):
            norm_2(1, r)

        def first_norm_3(r):
            norm_3(1, r, eps1)

        def first_norm_4(r):
            norm_4(1, r, z1[r], z1_bias)

        def first_norm_5(r):
            n1[r] = held.tile([P, PIECE], BF16, name="n1_%d" % r)
            norm_5(1, r, n1[r])

        z2, hid, result = {}, {}, {}

        def z2_bank(r, cols):
            return z2["rest"] if r == LAST and cols.start >= MAIN else z2[r]

        def second_norm_1(r, only=None):
            for cols in only or parts(2, r):
                norm_1(2, r, z2_bank(r, cols), z2_bias, [cols])

        def second_norm_2(r, only=None):
            norm_2(2, r, only)

        def second_norm_3(r, only=None):
            norm_3(2, r, eps2, only)

        def second_norm_4(r, only=None):
            for cols in only or parts(2, r):
                norm_4(2, r, z2_bank(r, cols), z2_bias, [cols])

        def second_norm_5(r, only=None):
            if r not in result:
                result[r] = work.tile([P, PIECE], F32, name="result")
            norm_5(2, r, result[r], only)
            for cols in only or parts(2, r):
                nc.sync.dma_start(out[:, piece(r)][:, cols], result[r][:, cols])

        def pause(r):
            pass

        def centred(vec, row, factor, name):
            total = held.tile([P, 1], F32, name=name + "_total")
            nc.vector.tensor_reduce(out=total[:], in_=row[:], axis=mybir.AxisListType.X, op=ALU.add)
            mean = held.tile([P, 1], F32, name=name + "_mean")
            nc.vector.tensor_scalar(out=mean[:], in0=total[:], scalar1=1.0 / P, scalar2=None, op0=ALU.mult)
            t = held.tile([P, 1], F32, name=name)
            nc.vector.tensor_scalar(
                out=t[:], in0=vec[:], scalar1=mean[:, 0:1], scalar2=factor, op0=ALU.subtract, op1=ALU.mult
            )
            return t

        def in_stream(r):
            return slice(0, MAIN if r == LAST else PIECE)

        def hidden_block(g):
            r, a = divmod(g, HID_BLOCKS)
            if r < N_PIECES:
                hid_ps = new_bank("hid_ps")
                nc.tensor.matmul(hid_ps[:], w1_sb[:, a : HID : HID_BLOCKS], n1[r][:], start=True, stop=True)
                if r == LAST:
                    hid[g] = held.tile([P, PIECE], BF16, name="hid_last%d" % a)
                else:
                    hid[g] = hidden.tile([P, PIECE], BF16, name="hid")
                if a % 2 == 0 or a == HID_BLOCKS - 1:
                    nc.scalar.activation(out=hid[g][:], in_=hid_ps[:], func=ACT.Relu, bias=b1_sb[:, a : a + 1])
                else:
                    nc.vector.tensor_scalar(
                        out=hid[g][:], in0=hid_ps[:], scalar1=b1_sb[:, a : a + 1], scalar2=0.0,
                        op0=ALU.add, op1=ALU.max,
                    )
            if g >= AHEAD:
                done_r, done_a = divmod(g - AHEAD, HID_BLOCKS)
                cols = in_stream(done_r)
                if done_a == 0:
                    z2[done_r] = new_bank("z2")
                    nc.tensor.matmul(z2[done_r][:, cols], center[:], n1[done_r][:, cols], start=True, stop=False)
                nc.tensor.matmul(
                    z2[done_r][:, cols], w2_c[:, done_a, :], hid[g - AHEAD][:, cols],
                    start=False, stop=(done_a == HID_BLOCKS - 1),
                )

        def rest_steps():
            z2["rest"] = new_bank("z2_rest")
            cols = slice(MAIN, PIECE)
            steps = [lambda: nc.tensor.matmul(z2["rest"][:, cols], center[:], n1[LAST][:, cols], start=True, stop=False)]
            for a in range(HID_BLOCKS):
                steps.append(
                    lambda a=a: nc.tensor.matmul(
                        z2["rest"][:, cols], w2_c[:, a, :], hid[LAST * HID_BLOCKS + a][:, cols],
                        start=False, stop=(a == HID_BLOCKS - 1),
                    )
                )
            return steps

        def open_bank(r, which, half):
            project_pos_half(banks[r, which], w_twice[which][:], r, half, start=True, stop=False)

        def close_bank(r, which):
            project_table(banks[r, which], w_sb[which][:], r, start=False, stop=True)
            finish(r, which)

        for r, which in second_run:
            banks[r, which] = new_bank("proj")
            open_bank(r, which, 0)
        flip_between(0, [lambda r=r, which=which: open_bank(r, which, 1) for r, which in second_run])
        flip_between(1, [lambda r=r, which=which: close_bank(r, which) for r, which in second_run])
        for u in range(EARLY_BAND, BLOCKS):
            band_weights(u)

        wo_sum = held.tile([P, 1], F32, name="wo_sum")
        nc.vector.tensor_reduce(out=wo_sum[:], in_=wo_sb[:], axis=mybir.AxisListType.X, op=ALU.add)
        wo_mean = held.tile([P, 1], F32, name="wo_mean")
        nc.vector.tensor_scalar(out=wo_mean[:], in0=wo_sum[:], scalar1=1.0 / P, scalar2=None, op0=ALU.mult)
        wo_c = held.tile([P, P], BF16, name="wo_c")
        nc.vector.tensor_scalar(out=wo_c[:], in0=wo_sb[:], scalar1=wo_mean[:, 0:1], scalar2=None, op0=ALU.subtract)

        flip_between(2, sum_steps(0))
        divide_1(0)
        flip_between(3, sum_steps(1))
        z1_bias = centred(bo_sb, bo_row, 1.0 / SC, "z1_bias")
        z2_bias = centred(b2_sb, b2_row, 1.0, "z2_bias")
        residual_pos(0)
        residual_pos(1)
        residual_pos(2)
        residual_table(0)
        residual_table(1)
        residual_table(2)
        divide_2(0)
        divide_3(0)
        divide_4(0)
        sums_of_2 = sum_steps(2)
        run(sums_of_2[:4])
        project_out(0)
        divide_1(1)
        first_norm_1(0)
        run(sums_of_2[4:10])
        first_norm_2(0)
        first_norm_3(0)
        divide_2(1)
        divide_3(1)
        first_norm_4(0)
        first_norm_5(0)
        run(sums_of_2[10:])
        run(sum_steps(3))
        divide_1(2)
        divide_1(3)

        w2_mean = held.tile([P, HID_BLOCKS], F32, name="w2_mean")
        w2_c = held.tile([P, HID_BLOCKS, P], BF16, name="w2_c")
        for a in range(0, HID_BLOCKS, 4):
            nc.vector.tensor_reduce(out=w2_mean[:, a : a + 4], in_=w2_sb[:, a : a + 4, :], axis=mybir.AxisListType.X, op=ALU.add)
        nc.vector.tensor_scalar(out=w2_mean[:], in0=w2_mean[:], scalar1=1.0 / P, scalar2=None, op0=ALU.mult)
        for a in range(HID_BLOCKS):
            nc.vector.tensor_scalar(
                out=w2_c[:, a, :], in0=w2_sb[:, a, :], scalar1=w2_mean[:, a : a + 1], scalar2=None, op0=ALU.subtract
            )

        def fold_steps(which_norm, eps):
            return (
                lambda r: fold_1(which_norm, r), lambda r: fold_2(which_norm, r), pause, pause, pause,
                lambda r: fold_3(which_norm, r), lambda r: fold_4(which_norm, r, eps), lambda r: fold_5(which_norm, r),
            )

        division = (divide_2, divide_3, divide_4)
        to_first_norm = (residual, project_out, first_norm_1)
        first_norm_soon = (pause, pause, first_norm_2, first_norm_3, first_norm_4, first_norm_5)
        first_norm_beside = fold_steps(1, eps1) + (first_norm_4, first_norm_5)
        second_norm_beside = (second_norm_1,) + fold_steps(2, eps2) + (second_norm_4, second_norm_5)
        divisions = [(divide_4, 1)] + [(step, r) for r in (2, 3) for step in division]
        mixing = [(pause, 2), (pause, 2)]
        mixing += [(step, 1) for step in (pause, pause, pause, project_out, first_norm_1) + first_norm_soon]
        mixing += [(step, 2) for step in to_first_norm + first_norm_beside if step is not residual]
        mixing += [(step, 3) for step in to_first_norm + first_norm_beside]
        norms = []
        rows = (divisions, mixing, norms)
        written = [0, 0, 0]
        for g in range(N_PIECES * HID_BLOCKS + AHEAD):
            hidden_block(g)
            done_r, done_a = divmod(g - AHEAD, HID_BLOCKS)
            if 0 <= done_r < LAST and done_a == HID_BLOCKS - 1:
                norms += [(step, done_r) for step in second_norm_beside]
            for i, row in enumerate(rows):
                if written[i] < len(row):
                    step, r = row[written[i]]
                    step(r)
                    written[i] += 1
        for i, row in enumerate(rows):
            for step, r in row[written[i] :]:
                step(r)

        first_half, second_half, rest = parts(2, LAST)
        rest_matmuls = rest_steps()
        third = len(rest_matmuls) // 3
        second_norm_1(LAST, [first_half, second_half])
        run(rest_matmuls[:third])
        second_norm_2(LAST, [first_half])
        run(rest_matmuls[third : 2 * third])
        second_norm_2(LAST, [second_half])
        run(rest_matmuls[2 * third :])
        for step in (second_norm_3, second_norm_4, second_norm_5):
            step(LAST, [first_half])
        for step in (second_norm_3, second_norm_4, second_norm_5):
            step(LAST, [second_half])
        for step in (second_norm_1, second_norm_2, second_norm_3, second_norm_4, second_norm_5):
            step(LAST, [rest])
